import numpy as np
import ml_dtypes


def mxq(x, axis, fmt="e4m3"):
    dtype, down = {"e4m3": (ml_dtypes.float8_e4m3fn, 7), "e5m2": (ml_dtypes.float8_e5m2, 14)}[fmt]
    v = np.moveaxis(np.asarray(x, np.float32).astype(ml_dtypes.bfloat16).astype(np.float64), axis, -1)
    blocks = v.reshape(v.shape[:-1] + (-1, 32))
    amax = np.abs(blocks).max(-1, keepdims=True)
    byte = np.maximum(np.where(amax > 0, np.frexp(amax)[1] - 1 + 127, 0) - down, 1)
    scale = np.exp2(byte - 127.0)
    codes = (blocks / scale).astype(np.float32).astype(dtype).astype(np.float64)
    return np.moveaxis((codes * scale).reshape(v.shape), -1, axis)


WIDE = False


def mx_kscale(k):
    if not WIDE:
        return np.ones(k)
    levels = np.array([10, -10, 5, -5, 0])
    if k % 512:
        return np.exp2(np.random.permutation(np.resize(levels, k // 32))).repeat(32)
    a = np.empty((k // 512, 16))
    for p in range(k // 512):
        a[p, :8] = np.random.permutation(np.resize(levels, 8))
        for g in range(8):
            far = levels[np.abs(levels - a[p, g]) >= 10]
            a[p, g + 8] = far[np.random.randint(len(far))]
    return np.exp2(a.ravel()).repeat(32)


BF16 = ml_dtypes.bfloat16


def bf(x):
    return np.asarray(x, np.float32).astype(BF16)


def f64(x):
    return np.asarray(x).astype(np.float64)


B, T, D = 2, 512, 1024
EPS_DENOM = 1e-6
EPS_LN = 1e-5


def elu1(z):
    return np.where(z > 0.0, z, np.exp(np.minimum(z, 0.0)) - 1.0) + 1.0


def layernorm(x, gamma, beta):
    mu = x.mean(axis=-1, keepdims=True)
    var = ((x - mu) ** 2).mean(axis=-1, keepdims=True)
    return (x - mu) * (1.0 / np.sqrt(var + EPS_LN)) * gamma + beta


def draw0():
    s, u = mx_kscale(D), mx_kscale(D)
    return {"q_feat": bf(elu1(np.random.standard_normal((B, T, D))) * s),
            "kv": bf(np.random.standard_normal((B, D, D)) * 0.45 * np.sqrt(T) / s[:, None] * u[None, :]),
            "k_sum": bf(T * (1.16 + 0.15 * np.random.standard_normal((B, D))) / s),
            "audio": bf(np.random.standard_normal((B, T, D))),
            "Wo": bf(np.random.standard_normal((D, D)) * 0.5 / np.sqrt(D) / u[None, :]),
            "bo": bf(np.random.standard_normal(D) * 0.2),
            "gamma": bf(1.0 + 0.1 * np.random.standard_normal(D)),
            "beta": bf(0.1 * np.random.standard_normal(D))}


def core(q_feat, kv, k_sum, audio, Wo, bo, gamma, beta):
    q = f64(q_feat)
    num = mxq(q, 2, "e4m3") @ mxq(f64(kv), 1, "e4m3")
    attn = num / (q * f64(k_sum)[:, None, :] + EPS_DENOM)
    y = (mxq(attn, 2, "e4m3") @ mxq(f64(Wo), 1, "e4m3").T) + f64(bo)
    return layernorm(f64(audio) + y, f64(gamma), f64(beta))


def e4m3fn_bytes(y):
    return np.clip(np.asarray(y, np.float64), -448.0, 448.0).astype(np.float32).astype(ml_dtypes.float8_e4m3fn).view(np.uint8)


def e4m3fn_values(b):
    return np.asarray(b, np.uint8).view(ml_dtypes.float8_e4m3fn).astype(np.float64)


def setup_inputs():
    d = draw0()
    x0 = np.asarray(d['Wo']).astype(np.float64)
    s = (np.max(np.abs(x0), axis=(0,), keepdims=True) / 448.0).astype(np.float32)
    out = {}
    for k, v in d.items():
        if k == 'Wo':
            out['Wo_bytes'] = e4m3fn_bytes(x0 / s.astype(np.float64))
            out['Wo_scale'] = s
        else:
            out[k] = v
    return out


def reference(q_feat, kv, k_sum, audio, Wo_bytes, Wo_scale, bo, gamma, beta):
    return core(q_feat, kv, k_sum, audio, e4m3fn_values(Wo_bytes) * Wo_scale.astype(np.float64), bo, gamma, beta)

@@ -1,0 +1,531 @@
+from contextlib import ExitStack
+
+import concourse.mybir as mybir
+from concourse.masks import make_identity
+
+B, T, D = 2, 512, 1024
+P = 128
+FLOPS = 2 * 2 * B * T * D * D
+
+F32 = mybir.dt.float32
+BF16 = mybir.dt.bfloat16
+U32 = mybir.dt.uint32
+U8 = mybir.dt.uint8
+FP8 = mybir.dt.float8_e4m3fn
+FP8X4 = mybir.dt.float8_e4m3fn_x4
+ALU = mybir.AluOpType
+ACT = mybir.ActivationFunctionType
+
+
+def words(ap):
+    return ap.bitcast(F32)
+
+
+def tile_linearattentionlayer_pb_kernel(tc, q_feat, kv, k_sum, audio, wo_bytes, wo_scale, bo, gamma, beta, out):
+    nc = tc.nc
+    with ExitStack() as ctx:
+        const = ctx.enter_context(tc.tile_pool(name="const", bufs=1))
+        work = ctx.enter_context(tc.tile_pool(name="work", bufs=2))
+        psum = ctx.enter_context(tc.psum_pool(name="psum", bufs=1))
+        ctx.enter_context(tc.manual_schedule())
+
+        q_raw, kv_raw, au_raw, wo8 = {}, {}, {}, {}
+
+        def load_q(b, h):
+            t_ = work.tile([P, 2, D], BF16, name="q_raw", bufs=3)
+            nc.sync.dma_start(out=t_[:], in_=q_feat[b, 256 * h : 256 * (h + 1), :].rearrange("(n p) k -> p n k", p=P))
+            q_raw[b, h] = t_
+
+        def load_kv(b, g, c):
+            src = kv[b].rearrange("(g p j) e -> g p j e", p=P, j=4)[g]
+            t_ = work.tile([P, 4, 512], BF16, name="kv_raw", bufs=5)
+            nc.sync.dma_start(out=t_[:], in_=src[:, :, 512 * c : 512 * (c + 1)])
+            kv_raw[b, g, c] = t_
+
+        def load_wo(h):
+            t_ = const.tile([P, 4, D], U8, name="wo8_%d" % h)
+            nc.sync.dma_start(out=t_[:], in_=wo_bytes[512 * h : 512 * (h + 1), :].rearrange("(r p) e -> p r e", p=P))
+            wo8[h] = t_
+
+        def load_audio(b, n):
+            t_ = work.tile([P, D], BF16, name="au", bufs=6)
+            nc.sync.dma_start(out=t_[:], in_=audio[b, P * n : P * (n + 1), :])
+            au_raw[b, n] = t_
+
+        srow = const.tile([P, D], F32, name="srow")
+        vec = const.tile([P, D], BF16, name="vec")
+        id_f = const.tile([P, P], F32, name="id_f")
+        id_b = const.tile([P, P], BF16, name="id_b")
+        ks_b = const.tile([P, 16], BF16, name="ks_b")
+        nc.vector.memset(srow[:], 0.0)
+        nc.vector.memset(vec[:], 0.0)
+        make_identity(nc, id_f[:])
+        make_identity(nc, id_b[:])
+        load_q(0, 0)
+        load_kv(0, 0, 0)
+        nc.sync.dma_start(out=srow[0:1, :], in_=wo_scale)
+        nc.sync.dma_start(out=ks_b[:].rearrange("p (b g t) -> p b g t", b=2, g=2), in_=k_sum.rearrange("b (g p t) -> p b g t", p=P, t=4))
+        load_q(0, 1)
+        load_wo(0)
+        load_kv(0, 1, 0)
+        for i, v in enumerate((bo, gamma, beta)):
+            nc.sync.dma_start(out=vec[i : i + 1, :], in_=v.unsqueeze(0))
+        load_kv(0, 0, 1)
+        load_kv(0, 1, 1)
+        load_wo(1)
+        load_q(1, 0)
+        load_q(1, 1)
+        for g, c in ((0, 0), (1, 0), (0, 1), (1, 1)):
+            load_kv(1, g, c)
+        for b in range(2):
+            for n in range(4):
+                load_audio(b, n)
+        ks_f = const.tile([P, 16], F32, name="ks_f")
+        eps = const.tile([P, 2], F32, name="eps")
+        nc.gpsimd.tensor_scalar(out=eps[:, 0:1], in0=id_f[:, 0:1], scalar1=0.0, scalar2=1e-6, op0=ALU.mult, op1=ALU.add)
+        nc.gpsimd.tensor_scalar(out=eps[:, 1:2], in0=id_f[:, 0:1], scalar1=0.0, scalar2=1e-5, op0=ALU.mult, op1=ALU.add)
+        nc.gpsimd.tensor_copy(out=ks_f[:], in_=ks_b[:])
+
+        gq, qc, qs = {}, {}, {}
+
+        xq = {}
+
+        def tqP(b, h, g):
+            xt = psum.tile([P, 2, 2, P], F32, name="tp", tag="bank", bufs=6)
+            xq[b, h, g] = xt
+            for n in range(2):
+                w = words(q_raw[b, h][:, n, :])
+                for u in range(2):
+                    nc.tensor.transpose(xt[:, n, u, :], w[:, 256 * g + u : 256 * (g + 1) : 2], id_f[:])
+
+        def tqS(b, h, g):
+            if h == 0:
+                gq[b, g] = work.tile([P, 2048], BF16, name="gq", bufs=3, align_bytes=64)
+            dst = words(gq[b, g][:, 1024 * h : 1024 * (h + 1)]).rearrange("p (n r u) -> p n r u", n=2, u=2)
+            nc.scalar.copy(out=dst, in_=xq[b, h, g][:].rearrange("p n u r -> p n r u"))
+
+        def qq(b, h, g):
+            if h == 0:
+                qc[b, g] = work.tile([P, 512], U32, name="qc", bufs=4, align_bytes=64)
+                qs[b, g] = work.tile([P, 512], U8, name="qs", bufs=4, align_bytes=64)
+            nc.vector.quantize_mx(out=qc[b, g][:, 256 * h : 256 * (h + 1)].bitcast(FP8X4), scales=qs[b, g][:, 256 * h : 256 * (h + 1)], in_=gq[b, g][:, 1024 * h : 1024 * (h + 1)])
+
+        kc, kss, grp = {}, {}, {}
+
+        def kv_tiles(b, g, c):
+            grp[b, g, c] = work.tile([P, 2048], BF16, name="kvg", bufs=3, align_bytes=64)
+
+        def kvV(b, g, c):
+            kv_tiles(b, g, c)
+            dst = grp[b, g, c][:].rearrange("p (t m j) -> p t m j", t=4, j=4)
+            nc.vector.tensor_copy(out=dst, in_=kv_raw[b, g, c][:].rearrange("p j (m t) -> p t m j", t=4))
+
+        def kvS(b, g, c):
+            kv_tiles(b, g, c)
+            dst = grp[b, g, c][:].rearrange("p (t m j) -> p t m j", t=4, j=4)
+            nc.scalar.copy(out=dst, in_=kv_raw[b, g, c][:].rearrange("p j (m t) -> p t m j", t=4))
+
+        ibs = {}
+
+        def kvP(b, g, c, k):
+            ib = psum.tile([P, D], BF16, name="ib", tag="bank", bufs=6)
+            src = kv_raw[b, g, c][:].rearrange("p j (m t) -> p t m j", t=4)
+            for t in range(2):
+                nc.tensor.matmul(ib[:, 512 * t : 512 * (t + 1)], id_b[:], src[:, 2 * k + t], start=True, stop=True)
+            ibs[b, g, c, k] = ib
+
+        def kvE(b, g, c, k):
+            if k == 0:
+                kv_tiles(b, g, c)
+            nc.scalar.copy(out=grp[b, g, c][:, 1024 * k : 1024 * (k + 1)], in_=ibs[b, g, c, k][:])
+
+        def kvF(b, g, c, k):
+            if k == 0:
+                kv_tiles(b, g, c)
+            nc.vector.tensor_copy(out=grp[b, g, c][:, 1024 * k : 1024 * (k + 1)], in_=ibs[b, g, c, k][:])
+
+        def kq(b, g, c):
+            if c == 0:
+                kc[b, g] = work.tile([P, D], U32, name="kc", bufs=4, align_bytes=64)
+                kss[b, g] = work.tile([P, D], U8, name="kss", bufs=4, align_bytes=64)
+            cs = slice(512 * c, 512 * (c + 1))
+            nc.vector.quantize_mx(out=kc[b, g][:, cs].bitcast(FP8X4), scales=kss[b, g][:, cs], in_=grp[b, g, c][:])
+
+        rr = {}
+
+        def ars(b, G, t):
+            if t == 0:
+                rr[b, G] = work.tile([P, 4, 512], F32, name="rr", bufs=3)
+            v = gq[b, G][:].rearrange("p (n j) -> p n j", j=4)
+            i = 8 * b + 4 * G + t
+            nc.scalar.activation(out=rr[b, G][:, t, :], in_=v[:, :, t], func=ACT.Abs_reciprocal_sqrt, bias=eps[:, 0:1], scale=ks_f[:, i : i + 1])
+
+        def sq(b, G, h):
+            r = rr[b, G][:, :, 256 * h : 256 * (h + 1)]
+            nc.scalar.activation(out=r, in_=r, func=ACT.Square)
+
+        at, ac, acs, num = {}, {}, {}, {}
+
+        def s1(b, n, G):
+            ns = slice(P * n, P * (n + 1))
+            num[b, n, G] = psum.tile([P, 4, P], F32, name="num", tag="bank", bufs=6)
+            for t in range(4):
+                cs = slice(512 * G + P * t, 512 * G + P * (t + 1))
+                for g in range(2):
+                    nc.tensor.matmul_mx(out=num[b, n, G][:, t, :], lhsT=kc[b, g][:, cs].bitcast(FP8X4), lhsT_scale=kss[b, g][:, cs], rhs=qc[b, g][:, ns].bitcast(FP8X4), rhs_scale=qs[b, g][:, ns], start=(g == 0), stop=(g == 1))
+
+        def mul(b, n, G):
+            ns = slice(P * n, P * (n + 1))
+            if n % 2 == 0:
+                at[b, n // 2, G] = work.tile([P, 1024], BF16, name="at", bufs=4, align_bytes=64)
+            nc.vector.tensor_tensor(out=at[b, n // 2, G][:, 512 * (n % 2) : 512 * (n % 2 + 1)].rearrange("p (n j) -> p n j", j=4), in0=num[b, n, G][:].rearrange("p j n -> p n j"), in1=rr[b, G][:, :, ns].rearrange("p j n -> p n j"), op=ALU.mult)
+
+        def aq(b, np_, G):
+            if np_ == 0:
+                ac[b, G] = work.tile([P, 512], U32, name="ac", bufs=4, align_bytes=64)
+                acs[b, G] = work.tile([P, 512], U8, name="acs", bufs=4, align_bytes=64)
+            ps = slice(256 * np_, 256 * (np_ + 1))
+            nc.vector.quantize_mx(out=ac[b, G][:, ps].bitcast(FP8X4), scales=acs[b, G][:, ps], in_=at[b, np_, G][:])
+
+        sc_bc = const.tile([P, D], F32, name="sc_bc")
+        bo_bc = const.tile([P, D], BF16, name="bo_bc")
+        be_bc = const.tile([P, D], BF16, name="be_bc")
+        gam = psum.tile([P, D], BF16, name="gam", bufs=1)
+        bep = psum.tile([P, D], BF16, name="bep", bufs=1)
+
+        spr = {}
+
+        def spsP(h):
+            hs = slice(512 * h, 512 * (h + 1))
+            spr[h] = psum.tile([P, 512], F32, name="sp", tag="bank", bufs=6)
+            nc.tensor.matmul(spr[h][:], id_f[:, 0:1].to_broadcast([P, P]), srow[:, hs], start=True, stop=True)
+
+        def spsS(h):
+            nc.scalar.copy(out=sc_bc[:, 512 * h : 512 * (h + 1)], in_=spr[h][:])
+
+        def spread_row(i, dst):
+            vb = gam if i == 1 else (bep if i == 2 else psum.tile([P, D], BF16, name="vb", tag="bank", bufs=6))
+            for h in range(2):
+                hs = slice(512 * h, 512 * (h + 1))
+                nc.tensor.matmul(vb[:, hs], id_b[:, i : i + 1].to_broadcast([P, P]), vec[:, hs], start=True, stop=True)
+            spr["v", i] = vb
+
+        def sprS(i, dst):
+            nc.scalar.copy(out=dst[:], in_=spr["v", i][:])
+
+        wc, wsc, gw, wb = {}, {}, {}, {}
+        for G in range(2):
+            wc[G] = const.tile([P, D], U32, name="wc%d" % G, align_bytes=64)
+            wsc[G] = const.tile([P, D], U8, name="wsc%d" % G, align_bytes=64)
+
+        def wo(r):
+            wb[r] = work.tile([P, D], BF16, name="wb", bufs=4)
+            nc.vector.tensor_tensor(out=wb[r][:], in0=wo8[r // 4][:, r % 4, :].bitcast(FP8), in1=sc_bc[:], op=ALU.mult)
+
+        def twP(rp, G):
+            xt = psum.tile([P, 2, 2, P], F32, name="tp", tag="bank", bufs=6)
+            xq[rp, G] = xt
+            for k in range(2):
+                for u in range(2):
+                    nc.tensor.transpose(xt[:, k, u, :], words(wb[2 * rp + k][:])[:, 256 * G + u : 256 * (G + 1) : 2], id_f[:])
+
+        def twS(rp, G):
+            i = rp % 2
+            if i == 0:
+                gw[rp // 2, G] = work.tile([P, 2048], BF16, name="gw", bufs=2, align_bytes=64)
+            dst = words(gw[rp // 2, G][:, 1024 * i : 1024 * (i + 1)]).rearrange("p (n r u) -> p n r u", n=2, u=2)
+            nc.scalar.copy(out=dst, in_=xq[rp, G][:].rearrange("p n u r -> p n r u"))
+
+        def wq(h, G):
+            hs = slice(512 * h, 512 * (h + 1))
+            nc.vector.quantize_mx(out=wc[G][:, hs].bitcast(FP8X4), scales=wsc[G][:, hs], in_=gw[h, G][:])
+
+        aa = {}
+
+        def res(b, n):
+            aa[b, n] = work.tile([P, D], F32, name="aa", bufs=4)
+            for h in range(2):
+                hs = slice(512 * h, 512 * (h + 1))
+                nc.gpsimd.tensor_tensor(out=aa[b, n][:, hs], in0=au_raw[b, n][:, hs], in1=bo_bc[:, hs], op=ALU.add)
+
+        def resV(b, n):
+            aa[b, n] = work.tile([P, D], F32, name="aa", bufs=4)
+            nc.vector.tensor_tensor(out=aa[b, n][:], in0=au_raw[b, n][:], in1=bo_bc[:], op=ALU.add)
+
+        y, x, xn, st, sv = {}, {}, {}, {}, {}
+
+        def s2(b, n):
+            ns = slice(P * n, P * (n + 1))
+            for h in range(2):
+                hs = slice(512 * h, 512 * (h + 1))
+                y[b, n, h] = psum.tile([P, 512], F32, name="y", tag="bank", bufs=6)
+                for G in range(2):
+                    nc.tensor.matmul_mx(out=y[b, n, h][:], lhsT=ac[b, G][:, ns].bitcast(FP8X4), lhsT_scale=acs[b, G][:, ns], rhs=wc[G][:, hs].bitcast(FP8X4), rhs_scale=wsc[G][:, hs], start=(G == 0), stop=(G == 1))
+
+        def addx(b, n):
+            x[b, n] = work.tile([P, D], F32, name="x", bufs=3)
+            st[b, n] = work.tile([P, 8], F32, name="st", bufs=4)
+            for h in range(2):
+                hs = slice(512 * h, 512 * (h + 1))
+                nc.vector.scalar_tensor_tensor(out=x[b, n][:, hs], in0=y[b, n, h][:], scalar=1.0, in1=aa[b, n][:, hs], op0=ALU.mult, op1=ALU.add, accum_out=st[b, n][:, h : h + 1])
+
+        def nmu(b, n):
+            nc.vector.tensor_scalar(out=st[b, n][:, 2:3], in0=st[b, n][:, 0:1], scalar1=st[b, n][:, 1:2], scalar2=-1.0 / D, op0=ALU.add, op1=ALU.mult)
+
+        def var(b, n):
+            sv[b, n] = work.tile([P, 8], F32, name="sv", bufs=4)
+            junk = work.tile([P, D], BF16, name="junk", bufs=2)
+            nc.scalar.activation(out=junk[:], in_=x[b, n][:], func=ACT.Square, bias=st[b, n][:, 2:3], accum_out=sv[b, n][:, 0:1])
+
+        def rstd(b, n):
+            nc.scalar.activation(out=sv[b, n][:, 1:2], in_=sv[b, n][:, 0:1], func=ACT.Abs_reciprocal_sqrt, bias=eps[:, 1:2], scale=1.0 / D)
+
+        def cgam(b, n):
+            xn[b, n] = work.tile([P, D], F32, name="xn", bufs=3)
+            nc.vector.scalar_tensor_tensor(out=xn[b, n][:], in0=x[b, n][:], scalar=st[b, n][:, 2:3], in1=gam[:], op0=ALU.add, op1=ALU.mult)
+
+        def srs(b, n):
+            nc.scalar.activation(out=xn[b, n][:], in_=xn[b, n][:], func=ACT.Copy, scale=sv[b, n][:, 1:2])
+
+        def dbeta(b, n):
+            for h in range(2):
+                hs = slice(512 * h, 512 * (h + 1))
+                nc.gpsimd.tensor_tensor(out=xn[b, n][:, hs], in0=xn[b, n][:, hs], in1=be_bc[:, hs], op=ALU.add)
+
+        def dV(b, n):
+            nc.vector.scalar_tensor_tensor(out=xn[b, n][:], in0=xn[b, n][:], scalar=sv[b, n][:, 1:2], in1=bep[:], op0=ALU.mult, op1=ALU.add)
+
+        def store(b, n):
+            nc.sync.dma_start(out=out[b, P * n : P * (n + 1), :], in_=xn[b, n][:])
+
+        kvV(0, 0, 0)
+        tqP(0, 0, 1)
+        tqS(0, 0, 1)
+        tqP(0, 0, 0)
+        tqS(0, 0, 0)
+        spsP(0)
+        kq(0, 0, 0)
+        spsP(1)
+        tqP(0, 1, 1)
+        spsS(0)
+        spsS(1)
+        tqP(0, 1, 0)
+        qq(0, 0, 0)
+        qq(0, 0, 1)
+        kvP(0, 1, 0, 0)
+        wo(1)
+        spread_row(0, bo_bc)
+        tqS(0, 1, 1)
+        kvP(0, 1, 0, 1)
+        wo(0)
+        kvE(0, 1, 0, 0)
+        twP(0, 1)
+        wo(3)
+        kvV(0, 0, 1)
+        kvE(0, 1, 0, 1)
+        ars(0, 1, 0)
+        wo(2)
+        twP(0, 0)
+        kvP(0, 1, 1, 1)
+        tqS(0, 1, 0)
+        ars(0, 1, 3)
+        kq(0, 1, 0)
+        tqP(1, 0, 0)
+        tqP(1, 1, 1)
+        wo(7)
+        spread_row(2, be_bc)
+        twS(0, 1)
+        kq(0, 0, 1)
+        qq(0, 1, 0)
+        wo(4)
+        sprS(0, bo_bc)
+        qq(0, 1, 1)
+        kvP(0, 1, 1, 0)
+        ars(0, 0, 0)
+        ars(0, 1, 2)
+        res(1, 1)
+        twP(1, 1)
+        ars(0, 1, 1)
+        kvE(0, 1, 1, 0)
+        kvE(0, 1, 1, 1)
+        twS(0, 0)
+        twP(1, 0)
+        twS(1, 1)
+        kq(0, 1, 1)
+        ars(0, 0, 2)
+        kvV(1, 0, 0)
+        s1(0, 0, 1)
+        twS(1, 0)
+        kvP(1, 1, 0, 1)
+        ars(0, 0, 1)
+        ars(0, 0, 3)
+        wo(5)
+        kvP(1, 1, 0, 0)
+        sq(0, 1, 0)
+        tqS(1, 0, 0)
+        tqP(1, 1, 0)
+        kvP(1, 1, 1, 0)
+        res(0, 2)
+        s1(0, 2, 0)
+        kvE(1, 1, 0, 0)
+        kq(1, 0, 0)
+        res(0, 0)
+        twP(2, 0)
+        sq(0, 0, 1)
+        kvE(1, 1, 0, 1)
+        wo(6)
+        kvE(1, 1, 1, 0)
+        mul(0, 0, 1)
+        s1(0, 2, 1)
+        s1(0, 1, 0)
+        wq(0, 0)
+        sq(0, 1, 1)
+        twS(2, 0)
+        s1(0, 0, 0)
+        sq(0, 0, 0)
+        res(0, 1)
+        kvS(1, 0, 1)
+        mul(0, 2, 0)
+        s1(0, 1, 1)
+        twP(2, 1)
+        twP(3, 0)
+        qq(1, 0, 0)
+        twS(3, 0)
+        tqS(1, 1, 0)
+        mul(0, 0, 0)
+        tqP(1, 0, 1)
+        mul(0, 1, 0)
+        mul(0, 1, 1)
+        mul(0, 2, 1)
+        wq(0, 1)
+        s1(0, 3, 1)
+        mul(0, 3, 1)
+        tqS(1, 0, 1)
+        qq(1, 0, 1)
+        kq(1, 1, 0)
+        twP(3, 1)
+        kvP(1, 1, 1, 1)
+        aq(0, 0, 1)
+        tqS(1, 1, 1)
+        qq(1, 1, 1)
+        twS(2, 1)
+        s1(1, 1, 0)
+        twS(3, 1)
+        wq(1, 0)
+        ars(1, 0, 0)
+        qq(1, 1, 0)
+        res(1, 2)
+        aq(0, 0, 0)
+        kvE(1, 1, 1, 1)
+        kq(1, 1, 1)
+        ars(1, 0, 2)
+        ars(1, 0, 1)
+        wq(1, 1)
+        res(1, 0)
+        ars(1, 0, 3)
+        s2(0, 0)
+        aq(0, 1, 1)
+        addx(0, 0)
+        s1(0, 3, 0)
+        ars(1, 1, 0)
+        ars(1, 1, 2)
+        s2(0, 1)
+        kq(1, 0, 1)
+        s1(1, 1, 1)
+        mul(0, 3, 0)
+        sprS(2, be_bc)
+        nmu(0, 0)
+        sq(1, 0, 0)
+        ars(1, 1, 3)
+        s1(1, 3, 1)
+        addx(0, 1)
+        res(0, 3)
+        aq(0, 1, 0)
+        ars(1, 1, 1)
+        spread_row(1, None)
+        var(0, 0)
+        sq(1, 1, 0)
+        s2(0, 2)
+        s1(1, 0, 0)
+        cgam(0, 0)
+        s1(1, 0, 1)
+        sq(1, 1, 1)
+        addx(0, 2)
+        s2(0, 3)
+        nmu(0, 1)
+        mul(1, 0, 0)
+        cgam(0, 1)
+        s1(1, 3, 0)
+        mul(1, 0, 1)
+        s1(1, 2, 0)
+        rstd(0, 0)
+        srs(0, 0)
+        nmu(0, 2)
+        mul(1, 1, 0)
+        mul(1, 1, 1)
+        aq(1, 0, 0)
+        s1(1, 2, 1)
+        var(0, 1)
+        cgam(0, 2)
+        aq(1, 0, 1)
+        addx(0, 3)
+        mul(1, 2, 1)
+        nmu(0, 3)
+        s2(1, 0)
+        var(0, 2)
+        s2(1, 1)
+        rstd(0, 2)
+        addx(1, 0)
+        rstd(0, 1)
+        srs(0, 1)
+        sq(1, 0, 1)
+        srs(0, 2)
+        var(0, 3)
+        dbeta(0, 0)
+        mul(1, 2, 0)
+        cgam(0, 3)
+        nmu(1, 0)
+        mul(1, 3, 0)
+        var(1, 0)
+        dbeta(0, 1)
+        mul(1, 3, 1)
+        store(0, 0)
+        rstd(0, 3)
+        srs(0, 3)
+        rstd(1, 0)
+        aq(1, 1, 0)
+        cgam(1, 0)
+        addx(1, 1)
+        aq(1, 1, 1)
+        store(0, 1)
+        nmu(1, 1)
+        s2(1, 3)
+        res(1, 3)
+        addx(1, 3)
+        dbeta(0, 2)
+        srs(1, 0)
+        s2(1, 2)
+        var(1, 1)
+        store(0, 2)
+        rstd(1, 1)
+        nmu(1, 3)
+        dbeta(0, 3)
+        var(1, 3)
+        cgam(1, 1)
+        store(0, 3)
+        rstd(1, 3)
+        addx(1, 2)
+        cgam(1, 3)
+        dbeta(1, 0)
+        nmu(1, 2)
+        store(1, 0)
+        dV(1, 3)
+        store(1, 3)
+        srs(1, 1)
+        dbeta(1, 1)
+        cgam(1, 2)
+        var(1, 2)
+        rstd(1, 2)
+        store(1, 1)
+        dV(1, 2)
+        store(1, 2)

@@ -48,29 +48,28 @@ def tile_linearattentionlayer_pb_kernel(tc, q_feat, kv, k_sum, audio, wo_bytes, 
             wo8[h] = t_
 
         def load_audio(b, n):
-            t_ = work.tile([P, D], BF16, name="au", bufs=6)
+            t_ = work.tile([P, D], BF16, name="au", bufs=4)
             nc.sync.dma_start(out=t_[:], in_=audio[b, P * n : P * (n + 1), :])
             au_raw[b, n] = t_
 
-        srow = const.tile([P, D], F32, name="srow")
+        scol = const.tile([P, 8], F32, name="scol")
         vec = const.tile([P, D], BF16, name="vec")
         id_f = const.tile([P, P], F32, name="id_f")
         id_b = const.tile([P, P], BF16, name="id_b")
         ks_b = const.tile([P, 16], BF16, name="ks_b")
-        nc.vector.memset(srow[:], 0.0)
         nc.vector.memset(vec[:], 0.0)
         make_identity(nc, id_f[:])
         make_identity(nc, id_b[:])
-        load_q(0, 0)
+        nc.sync.dma_start(out=scol[:], in_=wo_scale.rearrange("o (m p) -> p (o m)", p=P))
         load_kv(0, 0, 0)
-        nc.sync.dma_start(out=srow[0:1, :], in_=wo_scale)
         nc.sync.dma_start(out=ks_b[:].rearrange("p (b g t) -> p b g t", b=2, g=2), in_=k_sum.rearrange("b (g p t) -> p b g t", p=P, t=4))
+        load_q(0, 0)
         load_q(0, 1)
-        load_wo(0)
         load_kv(0, 1, 0)
+        load_kv(0, 0, 1)
+        load_wo(0)
         for i, v in enumerate((bo, gamma, beta)):
             nc.sync.dma_start(out=vec[i : i + 1, :], in_=v.unsqueeze(0))
-        load_kv(0, 0, 1)
         load_kv(0, 1, 1)
         load_wo(1)
         load_q(1, 0)
@@ -86,12 +85,12 @@ def tile_linearattentionlayer_pb_kernel(tc, q_feat, kv, k_sum, audio, wo_bytes, 
         nc.gpsimd.tensor_scalar(out=eps[:, 1:2], in0=id_f[:, 0:1], scalar1=0.0, scalar2=1e-5, op0=ALU.mult, op1=ALU.add)
         nc.gpsimd.tensor_copy(out=ks_f[:], in_=ks_b[:])
 
-        gq, qc, qs = {}, {}, {}
-
-        xq = {}
+        gq, qc, qs, xq = {}, {}, {}, {}
+        for b in range(2):
+            gq[b] = const.tile([P, 4096], BF16, name="gq%d" % b, align_bytes=64)
 
         def tqP(b, h, g):
-            xt = psum.tile([P, 2, 2, P], F32, name="tp", tag="bank", bufs=6)
+            xt = psum.tile([P, 2, 2, P], F32, name="tp", tag="bank", bufs=7)
             xq[b, h, g] = xt
             for n in range(2):
                 w = words(q_raw[b, h][:, n, :])
@@ -99,112 +98,99 @@ def tile_linearattentionlayer_pb_kernel(tc, q_feat, kv, k_sum, audio, wo_bytes, 
                     nc.tensor.transpose(xt[:, n, u, :], w[:, 256 * g + u : 256 * (g + 1) : 2], id_f[:])
 
         def tqS(b, h, g):
-            if h == 0:
-                gq[b, g] = work.tile([P, 2048], BF16, name="gq", bufs=3, align_bytes=64)
-            dst = words(gq[b, g][:, 1024 * h : 1024 * (h + 1)]).rearrange("p (n r u) -> p n r u", n=2, u=2)
+            o = 2048 * h + 1024 * g
+            dst = words(gq[b][:, o : o + 1024]).rearrange("p (n r u) -> p n r u", n=2, u=2)
             nc.scalar.copy(out=dst, in_=xq[b, h, g][:].rearrange("p n u r -> p n r u"))
 
-        def qq(b, h, g):
-            if h == 0:
-                qc[b, g] = work.tile([P, 512], U32, name="qc", bufs=4, align_bytes=64)
-                qs[b, g] = work.tile([P, 512], U8, name="qs", bufs=4, align_bytes=64)
-            nc.vector.quantize_mx(out=qc[b, g][:, 256 * h : 256 * (h + 1)].bitcast(FP8X4), scales=qs[b, g][:, 256 * h : 256 * (h + 1)], in_=gq[b, g][:, 1024 * h : 1024 * (h + 1)])
+        def qq(b, h):
+            qc[b, h] = work.tile([P, 512], U32, name="qc", bufs=4, align_bytes=64)
+            qs[b, h] = work.tile([P, 512], U8, name="qs", bufs=4, align_bytes=64)
+            nc.vector.quantize_mx(out=qc[b, h][:].bitcast(FP8X4), scales=qs[b, h][:], in_=gq[b][:, 2048 * h : 2048 * (h + 1)])
 
-        kc, kss, grp = {}, {}, {}
+        kc, kss, grp, ibs = {}, {}, {}, {}
 
-        def kv_tiles(b, g, c):
-            grp[b, g, c] = work.tile([P, 2048], BF16, name="kvg", bufs=3, align_bytes=64)
+        def kv_dst(b, g, c):
+            if (b, c) not in grp:
+                grp[b, c] = work.tile([P, 4096], BF16, name="kvg", bufs=2, align_bytes=64)
+            return grp[b, c][:, 2048 * g : 2048 * (g + 1)]
 
         def kvV(b, g, c):
-            kv_tiles(b, g, c)
-            dst = grp[b, g, c][:].rearrange("p (t m j) -> p t m j", t=4, j=4)
+            dst = kv_dst(b, g, c).rearrange("p (t m j) -> p t m j", t=4, j=4)
             nc.vector.tensor_copy(out=dst, in_=kv_raw[b, g, c][:].rearrange("p j (m t) -> p t m j", t=4))
 
         def kvS(b, g, c):
-            kv_tiles(b, g, c)
-            dst = grp[b, g, c][:].rearrange("p (t m j) -> p t m j", t=4, j=4)
+            dst = kv_dst(b, g, c).rearrange("p (t m j) -> p t m j", t=4, j=4)
             nc.scalar.copy(out=dst, in_=kv_raw[b, g, c][:].rearrange("p j (m t) -> p t m j", t=4))
 
-        ibs = {}
-
         def kvP(b, g, c, k):
-            ib = psum.tile([P, D], BF16, name="ib", tag="bank", bufs=6)
+            ib = psum.tile([P, D], BF16, name="ib", tag="bank", bufs=7)
             src = kv_raw[b, g, c][:].rearrange("p j (m t) -> p t m j", t=4)
             for t in range(2):
                 nc.tensor.matmul(ib[:, 512 * t : 512 * (t + 1)], id_b[:], src[:, 2 * k + t], start=True, stop=True)
             ibs[b, g, c, k] = ib
 
         def kvE(b, g, c, k):
-            if k == 0:
-                kv_tiles(b, g, c)
-            nc.scalar.copy(out=grp[b, g, c][:, 1024 * k : 1024 * (k + 1)], in_=ibs[b, g, c, k][:])
+            nc.scalar.copy(out=kv_dst(b, g, c)[:, 1024 * k : 1024 * (k + 1)], in_=ibs[b, g, c, k][:])
 
         def kvF(b, g, c, k):
-            if k == 0:
-                kv_tiles(b, g, c)
-            nc.vector.tensor_copy(out=grp[b, g, c][:, 1024 * k : 1024 * (k + 1)], in_=ibs[b, g, c, k][:])
+            nc.vector.tensor_copy(out=kv_dst(b, g, c)[:, 1024 * k : 1024 * (k + 1)], in_=ibs[b, g, c, k][:])
 
-        def kq(b, g, c):
-            if c == 0:
-                kc[b, g] = work.tile([P, D], U32, name="kc", bufs=4, align_bytes=64)
-                kss[b, g] = work.tile([P, D], U8, name="kss", bufs=4, align_bytes=64)
-            cs = slice(512 * c, 512 * (c + 1))
-            nc.vector.quantize_mx(out=kc[b, g][:, cs].bitcast(FP8X4), scales=kss[b, g][:, cs], in_=grp[b, g, c][:])
+        def kq(b, c):
+            kc[b, c] = work.tile([P, D], U32, name="kc", bufs=4, align_bytes=64)
+            kss[b, c] = work.tile([P, D], U8, name="kss", bufs=4, align_bytes=64)
+            nc.vector.quantize_mx(out=kc[b, c][:].bitcast(FP8X4), scales=kss[b, c][:], in_=grp[b, c][:])
 
         rr = {}
 
         def ars(b, G, t):
-            if t == 0:
-                rr[b, G] = work.tile([P, 4, 512], F32, name="rr", bufs=3)
-            v = gq[b, G][:].rearrange("p (n j) -> p n j", j=4)
-            i = 8 * b + 4 * G + t
-            nc.scalar.activation(out=rr[b, G][:, t, :], in_=v[:, :, t], func=ACT.Abs_reciprocal_sqrt, bias=eps[:, 0:1], scale=ks_f[:, i : i + 1])
+            if b not in rr:
+                rr[b] = work.tile([P, 8, 512], F32, name="rr", bufs=2)
+            v = gq[b][:].rearrange("p (h g n j) -> p h g n j", h=2, g=2, j=4)
+            i = 4 * G + t
+            nc.scalar.activation(out=rr[b][:, i, :].rearrange("p (h n) -> p h n", h=2), in_=v[:, :, G, :, t], func=ACT.Abs_reciprocal_sqrt, bias=eps[:, 0:1], scale=ks_f[:, 8 * b + i : 8 * b + i + 1])
 
-        def sq(b, G, h):
-            r = rr[b, G][:, :, 256 * h : 256 * (h + 1)]
+        def sq(b, h):
+            r = rr[b][:, :, 256 * h : 256 * (h + 1)]
             nc.scalar.activation(out=r, in_=r, func=ACT.Square)
 
         at, ac, acs, num = {}, {}, {}, {}
 
         def s1(b, n, G):
-            ns = slice(P * n, P * (n + 1))
-            num[b, n, G] = psum.tile([P, 4, P], F32, name="num", tag="bank", bufs=6)
+            num[b, n, G] = psum.tile([P, 4, P], F32, name="num", tag="bank", bufs=7)
             for t in range(4):
-                cs = slice(512 * G + P * t, 512 * G + P * (t + 1))
                 for g in range(2):
-                    nc.tensor.matmul_mx(out=num[b, n, G][:, t, :], lhsT=kc[b, g][:, cs].bitcast(FP8X4), lhsT_scale=kss[b, g][:, cs], rhs=qc[b, g][:, ns].bitcast(FP8X4), rhs_scale=qs[b, g][:, ns], start=(g == 0), stop=(g == 1))
+                    cs = slice(512 * g + P * t, 512 * g + P * (t + 1))
+                    o = 256 * g + P * (n % 2)
+                    nc.tensor.matmul_mx(out=num[b, n, G][:, t, :], lhsT=kc[b, G][:, cs].bitcast(FP8X4), lhsT_scale=kss[b, G][:, cs], rhs=qc[b, n // 2][:, o : o + P].bitcast(FP8X4), rhs_scale=qs[b, n // 2][:, o : o + P], start=(g == 0), stop=(g == 1))
 
         def mul(b, n, G):
             ns = slice(P * n, P * (n + 1))
-            if n % 2 == 0:
-                at[b, n // 2, G] = work.tile([P, 1024], BF16, name="at", bufs=4, align_bytes=64)
-            nc.vector.tensor_tensor(out=at[b, n // 2, G][:, 512 * (n % 2) : 512 * (n % 2 + 1)].rearrange("p (n j) -> p n j", j=4), in0=num[b, n, G][:].rearrange("p j n -> p n j"), in1=rr[b, G][:, :, ns].rearrange("p j n -> p n j"), op=ALU.mult)
+            if (b, n // 2) not in at:
+                at[b, n // 2] = work.tile([P, 2048], BF16, name="at", bufs=2, align_bytes=64)
+            o = 1024 * G + 512 * (n % 2)
+            nc.vector.tensor_tensor(out=at[b, n // 2][:, o : o + 512].rearrange("p (n j) -> p n j", j=4), in0=num[b, n, G][:].rearrange("p j n -> p n j"), in1=rr[b][:, 4 * G : 4 * (G + 1), ns].rearrange("p j n -> p n j"), op=ALU.mult)
 
-        def aq(b, np_, G):
-            if np_ == 0:
-                ac[b, G] = work.tile([P, 512], U32, name="ac", bufs=4, align_bytes=64)
-                acs[b, G] = work.tile([P, 512], U8, name="acs", bufs=4, align_bytes=64)
-            ps = slice(256 * np_, 256 * (np_ + 1))
-            nc.vector.quantize_mx(out=ac[b, G][:, ps].bitcast(FP8X4), scales=acs[b, G][:, ps], in_=at[b, np_, G][:])
+        def aq(b, h):
+            ac[b, h] = work.tile([P, 512], U32, name="ac", bufs=4, align_bytes=64)
+            acs[b, h] = work.tile([P, 512], U8, name="acs", bufs=4, align_bytes=64)
+            nc.vector.quantize_mx(out=ac[b, h][:].bitcast(FP8X4), scales=acs[b, h][:], in_=at[b, h][:])
 
         sc_bc = const.tile([P, D], F32, name="sc_bc")
         bo_bc = const.tile([P, D], BF16, name="bo_bc")
         be_bc = const.tile([P, D], BF16, name="be_bc")
         gam = psum.tile([P, D], BF16, name="gam", bufs=1)
-        bep = psum.tile([P, D], BF16, name="bep", bufs=1)
-
         spr = {}
 
         def spsP(h):
-            hs = slice(512 * h, 512 * (h + 1))
-            spr[h] = psum.tile([P, 512], F32, name="sp", tag="bank", bufs=6)
-            nc.tensor.matmul(spr[h][:], id_f[:, 0:1].to_broadcast([P, P]), srow[:, hs], start=True, stop=True)
+            spr[h] = psum.tile([P, 512], F32, name="sp", tag="bank", bufs=7)
+            for m in range(4):
+                nc.tensor.matmul(spr[h][:, P * m : P * (m + 1)], scol[:, 4 * h + m : 4 * h + m + 1].to_broadcast([P, P]), id_f[:], start=True, stop=True)
 
         def spsS(h):
             nc.scalar.copy(out=sc_bc[:, 512 * h : 512 * (h + 1)], in_=spr[h][:])
 
         def spread_row(i, dst):
-            vb = gam if i == 1 else (bep if i == 2 else psum.tile([P, D], BF16, name="vb", tag="bank", bufs=6))
+            vb = gam if i == 1 else psum.tile([P, D], BF16, name="vb", tag="bank", bufs=7)
             for h in range(2):
                 hs = slice(512 * h, 512 * (h + 1))
                 nc.tensor.matmul(vb[:, hs], id_b[:, i : i + 1].to_broadcast([P, P]), vec[:, hs], start=True, stop=True)
@@ -214,53 +200,53 @@ def tile_linearattentionlayer_pb_kernel(tc, q_feat, kv, k_sum, audio, wo_bytes, 
             nc.scalar.copy(out=dst[:], in_=spr["v", i][:])
 
         wc, wsc, gw, wb = {}, {}, {}, {}
-        for G in range(2):
-            wc[G] = const.tile([P, D], U32, name="wc%d" % G, align_bytes=64)
-            wsc[G] = const.tile([P, D], U8, name="wsc%d" % G, align_bytes=64)
 
         def wo(r):
             wb[r] = work.tile([P, D], BF16, name="wb", bufs=4)
             nc.vector.tensor_tensor(out=wb[r][:], in0=wo8[r // 4][:, r % 4, :].bitcast(FP8), in1=sc_bc[:], op=ALU.mult)
 
         def twP(rp, G):
-            xt = psum.tile([P, 2, 2, P], F32, name="tp", tag="bank", bufs=6)
+            xt = psum.tile([P, 2, 2, P], F32, name="tp", tag="bank", bufs=7)
             xq[rp, G] = xt
             for k in range(2):
                 for u in range(2):
                     nc.tensor.transpose(xt[:, k, u, :], words(wb[2 * rp + k][:])[:, 256 * G + u : 256 * (G + 1) : 2], id_f[:])
 
         def twS(rp, G):
-            i = rp % 2
-            if i == 0:
-                gw[rp // 2, G] = work.tile([P, 2048], BF16, name="gw", bufs=2, align_bytes=64)
-            dst = words(gw[rp // 2, G][:, 1024 * i : 1024 * (i + 1)]).rearrange("p (n r u) -> p n r u", n=2, u=2)
+            h, i = rp // 2, rp % 2
+            if h not in gw:
+                gw[h] = work.tile([P, 4096], BF16, name="gw", bufs=1, align_bytes=64)
+            o = 2048 * G + 1024 * i
+            dst = words(gw[h][:, o : o + 1024]).rearrange("p (n r u) -> p n r u", n=2, u=2)
             nc.scalar.copy(out=dst, in_=xq[rp, G][:].rearrange("p n u r -> p n r u"))
 
-        def wq(h, G):
-            hs = slice(512 * h, 512 * (h + 1))
-            nc.vector.quantize_mx(out=wc[G][:, hs].bitcast(FP8X4), scales=wsc[G][:, hs], in_=gw[h, G][:])
+        def wq(h):
+            wc[h] = const.tile([P, D], U32, name="wc%d" % h, align_bytes=64)
+            wsc[h] = const.tile([P, D], U8, name="wsc%d" % h, align_bytes=64)
+            nc.vector.quantize_mx(out=wc[h][:].bitcast(FP8X4), scales=wsc[h][:], in_=gw[h][:])
 
         aa = {}
 
         def res(b, n):
-            aa[b, n] = work.tile([P, D], F32, name="aa", bufs=4)
+            aa[b, n] = work.tile([P, D], F32, name="aa", bufs=3)
             for h in range(2):
                 hs = slice(512 * h, 512 * (h + 1))
                 nc.gpsimd.tensor_tensor(out=aa[b, n][:, hs], in0=au_raw[b, n][:, hs], in1=bo_bc[:, hs], op=ALU.add)
 
         def resV(b, n):
-            aa[b, n] = work.tile([P, D], F32, name="aa", bufs=4)
+            aa[b, n] = work.tile([P, D], F32, name="aa", bufs=3)
             nc.vector.tensor_tensor(out=aa[b, n][:], in0=au_raw[b, n][:], in1=bo_bc[:], op=ALU.add)
 
         y, x, xn, st, sv = {}, {}, {}, {}, {}
 
         def s2(b, n):
-            ns = slice(P * n, P * (n + 1))
+            o = P * (n % 2)
             for h in range(2):
-                hs = slice(512 * h, 512 * (h + 1))
-                y[b, n, h] = psum.tile([P, 512], F32, name="y", tag="bank", bufs=6)
+                y[b, n, h] = psum.tile([P, 512], F32, name="y", tag="bank", bufs=7)
                 for G in range(2):
-                    nc.tensor.matmul_mx(out=y[b, n, h][:], lhsT=ac[b, G][:, ns].bitcast(FP8X4), lhsT_scale=acs[b, G][:, ns], rhs=wc[G][:, hs].bitcast(FP8X4), rhs_scale=wsc[G][:, hs], start=(G == 0), stop=(G == 1))
+                    ts = slice(256 * G + o, 256 * G + o + P)
+                    ws = slice(512 * G, 512 * (G + 1))
+                    nc.tensor.matmul_mx(out=y[b, n, h][:], lhsT=ac[b, n // 2][:, ts].bitcast(FP8X4), lhsT_scale=acs[b, n // 2][:, ts], rhs=wc[h][:, ws].bitcast(FP8X4), rhs_scale=wsc[h][:, ws], start=(G == 0), stop=(G == 1))
 
         def addx(b, n):
             x[b, n] = work.tile([P, D], F32, name="x", bufs=3)
@@ -274,7 +260,7 @@ def tile_linearattentionlayer_pb_kernel(tc, q_feat, kv, k_sum, audio, wo_bytes, 
 
         def var(b, n):
             sv[b, n] = work.tile([P, 8], F32, name="sv", bufs=4)
-            junk = work.tile([P, D], BF16, name="junk", bufs=2)
+            junk = work.tile([P, D], BF16, name="junk", bufs=1)
             nc.scalar.activation(out=junk[:], in_=x[b, n][:], func=ACT.Square, bias=st[b, n][:, 2:3], accum_out=sv[b, n][:, 0:1])
 
         def rstd(b, n):
@@ -293,239 +279,221 @@ def tile_linearattentionlayer_pb_kernel(tc, q_feat, kv, k_sum, audio, wo_bytes, 
                 nc.gpsimd.tensor_tensor(out=xn[b, n][:, hs], in0=xn[b, n][:, hs], in1=be_bc[:, hs], op=ALU.add)
 
         def dV(b, n):
-            nc.vector.scalar_tensor_tensor(out=xn[b, n][:], in0=xn[b, n][:], scalar=sv[b, n][:, 1:2], in1=bep[:], op0=ALU.mult, op1=ALU.add)
+            nc.vector.scalar_tensor_tensor(out=xn[b, n][:], in0=xn[b, n][:], scalar=sv[b, n][:, 1:2], in1=be_bc[:], op0=ALU.mult, op1=ALU.add)
 
         def store(b, n):
             nc.sync.dma_start(out=out[b, P * n : P * (n + 1), :], in_=xn[b, n][:])
 
         kvV(0, 0, 0)
-        tqP(0, 0, 1)
-        tqS(0, 0, 1)
-        tqP(0, 0, 0)
-        tqS(0, 0, 0)
         spsP(0)
-        kq(0, 0, 0)
-        spsP(1)
-        tqP(0, 1, 1)
         spsS(0)
+        tqP(0, 0, 1)
+        tqP(0, 0, 0)
+        spsP(1)
+        tqS(0, 0, 1)
+        tqP(0, 1, 1)
+        tqS(0, 0, 0)
         spsS(1)
         tqP(0, 1, 0)
-        qq(0, 0, 0)
-        qq(0, 0, 1)
-        kvP(0, 1, 0, 0)
-        wo(1)
-        spread_row(0, bo_bc)
         tqS(0, 1, 1)
-        kvP(0, 1, 0, 1)
-        wo(0)
-        kvE(0, 1, 0, 0)
-        twP(0, 1)
-        wo(3)
-        kvV(0, 0, 1)
-        kvE(0, 1, 0, 1)
-        ars(0, 1, 0)
-        wo(2)
-        twP(0, 0)
-        kvP(0, 1, 1, 1)
         tqS(0, 1, 0)
-        ars(0, 1, 3)
-        kq(0, 1, 0)
-        tqP(1, 0, 0)
-        tqP(1, 1, 1)
-        wo(7)
-        spread_row(2, be_bc)
-        twS(0, 1)
-        kq(0, 0, 1)
-        qq(0, 1, 0)
-        wo(4)
-        sprS(0, bo_bc)
-        qq(0, 1, 1)
+        kvP(0, 1, 0, 0)
+        kvP(0, 1, 0, 1)
+        qq(0, 0)
+        kvV(0, 0, 1)
         kvP(0, 1, 1, 0)
         ars(0, 0, 0)
-        ars(0, 1, 2)
-        res(1, 1)
-        twP(1, 1)
-        ars(0, 1, 1)
-        kvE(0, 1, 1, 0)
-        kvE(0, 1, 1, 1)
-        twS(0, 0)
-        twP(1, 0)
-        twS(1, 1)
-        kq(0, 1, 1)
+        wo(0)
         ars(0, 0, 2)
-        kvV(1, 0, 0)
-        s1(0, 0, 1)
-        twS(1, 0)
-        kvP(1, 1, 0, 1)
-        ars(0, 0, 1)
+        wo(1)
         ars(0, 0, 3)
-        wo(5)
-        kvP(1, 1, 0, 0)
-        sq(0, 1, 0)
-        tqS(1, 0, 0)
-        tqP(1, 1, 0)
-        kvP(1, 1, 1, 0)
-        res(0, 2)
-        s1(0, 2, 0)
-        kvE(1, 1, 0, 0)
-        kq(1, 0, 0)
-        res(0, 0)
-        twP(2, 0)
-        sq(0, 0, 1)
-        kvE(1, 1, 0, 1)
-        wo(6)
-        kvE(1, 1, 1, 0)
-        mul(0, 0, 1)
-        s1(0, 2, 1)
-        s1(0, 1, 0)
-        wq(0, 0)
-        sq(0, 1, 1)
-        twS(2, 0)
-        s1(0, 0, 0)
-        sq(0, 0, 0)
-        res(0, 1)
-        kvS(1, 0, 1)
-        mul(0, 2, 0)
-        s1(0, 1, 1)
-        twP(2, 1)
-        twP(3, 0)
-        qq(1, 0, 0)
-        twS(3, 0)
-        tqS(1, 1, 0)
-        mul(0, 0, 0)
+        ars(0, 1, 0)
+        ars(0, 0, 1)
+        ars(0, 1, 2)
+        ars(0, 1, 1)
+        twP(0, 1)
+        twP(0, 0)
+        kvP(0, 1, 1, 1)
+        twS(0, 0)
+        kvE(0, 1, 0, 1)
+        wo(3)
+        wo(2)
+        kvE(0, 1, 0, 0)
         tqP(1, 0, 1)
-        mul(0, 1, 0)
-        mul(0, 1, 1)
-        mul(0, 2, 1)
-        wq(0, 1)
-        s1(0, 3, 1)
-        mul(0, 3, 1)
-        tqS(1, 0, 1)
-        qq(1, 0, 1)
-        kq(1, 1, 0)
-        twP(3, 1)
-        kvP(1, 1, 1, 1)
-        aq(0, 0, 1)
+        kvE(0, 1, 1, 0)
+        twP(1, 1)
+        kvE(0, 1, 1, 1)
+        wo(7)
+        twS(0, 1)
+        tqP(1, 1, 1)
+        twP(1, 0)
+        wo(4)
+        tqP(1, 0, 0)
         tqS(1, 1, 1)
-        qq(1, 1, 1)
-        twS(2, 1)
-        s1(1, 1, 0)
-        twS(3, 1)
-        wq(1, 0)
-        ars(1, 0, 0)
-        qq(1, 1, 0)
-        res(1, 2)
-        aq(0, 0, 0)
-        kvE(1, 1, 1, 1)
-        kq(1, 1, 1)
-        ars(1, 0, 2)
-        ars(1, 0, 1)
-        wq(1, 1)
-        res(1, 0)
-        ars(1, 0, 3)
-        s2(0, 0)
-        aq(0, 1, 1)
-        addx(0, 0)
-        s1(0, 3, 0)
+        tqP(1, 1, 0)
+        kq(0, 1)
+        ars(0, 1, 3)
+        wo(6)
+        spread_row(0, bo_bc)
+        twP(3, 0)
+        twS(1, 1)
+        tqS(1, 1, 0)
+        kvP(1, 1, 0, 0)
+        tqS(1, 0, 0)
+        qq(0, 1)
+        kvP(1, 1, 0, 1)
+        twP(3, 1)
+        tqS(1, 0, 1)
+        s1(0, 1, 1)
+        twS(1, 0)
+        sprS(0, bo_bc)
+        kq(0, 0)
+        kvP(1, 1, 1, 0)
+        s1(0, 1, 0)
+        kvV(1, 0, 0)
+        resV(0, 1)
         ars(1, 1, 0)
-        ars(1, 1, 2)
-        s2(0, 1)
-        kq(1, 0, 1)
-        s1(1, 1, 1)
-        mul(0, 3, 0)
-        sprS(2, be_bc)
-        nmu(0, 0)
-        sq(1, 0, 0)
+        kvE(1, 1, 0, 1)
+        qq(1, 1)
+        ars(1, 0, 0)
+        kvE(1, 1, 0, 0)
+        s1(0, 0, 0)
+        qq(1, 0)
+        ars(1, 0, 1)
+        s1(0, 2, 0)
+        sq(0, 0)
+        wq(0)
+        wo(5)
+        resV(0, 0)
+        s1(0, 0, 1)
+        mul(0, 1, 1)
         ars(1, 1, 3)
-        s1(1, 3, 1)
-        addx(0, 1)
-        res(0, 3)
-        aq(0, 1, 0)
-        ars(1, 1, 1)
+        kvE(1, 1, 1, 0)
+        twS(3, 1)
+        sq(0, 1)
+        ars(1, 0, 2)
+        twS(3, 0)
+        kq(1, 0)
+        ars(1, 1, 2)
+        kvV(1, 0, 1)
+        s1(0, 2, 1)
+        res(1, 1)
+        kvP(1, 1, 1, 1)
+        mul(0, 2, 1)
+        spread_row(2, be_bc)
+        kvE(1, 1, 1, 1)
+        mul(0, 1, 0)
+        twP(2, 1)
+        twP(2, 0)
+        s1(0, 3, 1)
+        twS(2, 1)
+        twS(2, 0)
+        mul(0, 0, 1)
+        mul(0, 0, 0)
+        mul(0, 2, 0)
+        aq(0, 0)
+        wq(1)
         spread_row(1, None)
-        var(0, 0)
-        sq(1, 1, 0)
-        s2(0, 2)
-        s1(1, 0, 0)
-        cgam(0, 0)
-        s1(1, 0, 1)
-        sq(1, 1, 1)
-        addx(0, 2)
-        s2(0, 3)
-        nmu(0, 1)
-        mul(1, 0, 0)
-        cgam(0, 1)
+        s2(0, 1)
+        kq(1, 1)
+        sprS(2, be_bc)
+        ars(1, 1, 1)
+        addx(0, 1)
+        s2(0, 0)
+        s1(1, 1, 1)
+        ars(1, 0, 3)
+        sq(1, 1)
+        s1(0, 3, 0)
+        res(0, 2)
+        sq(1, 0)
+        mul(0, 3, 1)
         s1(1, 3, 0)
-        mul(1, 0, 1)
+        res(0, 3)
+        nmu(0, 1)
+        mul(0, 3, 0)
+        s1(1, 3, 1)
+        var(0, 1)
+        s1(1, 0, 0)
+        addx(0, 0)
+        rstd(0, 1)
+        aq(0, 1)
+        cgam(0, 1)
+        s2(0, 2)
+        addx(0, 2)
+        srs(0, 1)
+        s1(1, 2, 1)
+        mul(1, 0, 0)
+        nmu(0, 2)
         s1(1, 2, 0)
+        s1(1, 1, 0)
+        s2(0, 3)
+        mul(1, 3, 0)
+        s1(1, 0, 1)
+        mul(1, 3, 1)
+        addx(0, 3)
+        var(0, 2)
+        dbeta(0, 1)
+        store(0, 1)
+        mul(1, 2, 0)
+        res(1, 2)
+        mul(1, 2, 1)
+        rstd(0, 2)
+        nmu(0, 3)
+        var(0, 3)
+        cgam(0, 2)
+        mul(1, 1, 1)
+        mul(1, 0, 1)
+        mul(1, 1, 0)
+        srs(0, 2)
+        nmu(0, 0)
+        cgam(0, 3)
+        rstd(0, 3)
+        aq(1, 1)
+        cgam(0, 0)
+        aq(1, 0)
+        s2(1, 2)
+        s2(1, 1)
+        addx(1, 2)
+        nmu(1, 2)
+        var(0, 0)
+        res(1, 0)
+        srs(0, 3)
+        addx(1, 1)
+        dbeta(0, 2)
         rstd(0, 0)
         srs(0, 0)
-        nmu(0, 2)
-        mul(1, 1, 0)
-        mul(1, 1, 1)
-        aq(1, 0, 0)
-        s1(1, 2, 1)
-        var(0, 1)
-        cgam(0, 2)
-        aq(1, 0, 1)
-        addx(0, 3)
-        mul(1, 2, 1)
-        nmu(0, 3)
-        s2(1, 0)
-        var(0, 2)
-        s2(1, 1)
-        rstd(0, 2)
-        addx(1, 0)
-        rstd(0, 1)
-        srs(0, 1)
-        sq(1, 0, 1)
-        srs(0, 2)
-        var(0, 3)
-        dbeta(0, 0)
-        mul(1, 2, 0)
-        cgam(0, 3)
-        nmu(1, 0)
-        mul(1, 3, 0)
-        var(1, 0)
-        dbeta(0, 1)
-        mul(1, 3, 1)
-        store(0, 0)
-        rstd(0, 3)
-        srs(0, 3)
-        rstd(1, 0)
-        aq(1, 1, 0)
-        cgam(1, 0)
-        addx(1, 1)
-        aq(1, 1, 1)
-        store(0, 1)
-        nmu(1, 1)
-        s2(1, 3)
-        res(1, 3)
-        addx(1, 3)
-        dbeta(0, 2)
-        srs(1, 0)
-        s2(1, 2)
-        var(1, 1)
-        store(0, 2)
-        rstd(1, 1)
-        nmu(1, 3)
-        dbeta(0, 3)
-        var(1, 3)
-        cgam(1, 1)
-        store(0, 3)
-        rstd(1, 3)
-        addx(1, 2)
-        cgam(1, 3)
-        dbeta(1, 0)
-        nmu(1, 2)
-        store(1, 0)
-        dV(1, 3)
-        store(1, 3)
-        srs(1, 1)
-        dbeta(1, 1)
-        cgam(1, 2)
         var(1, 2)
+        s2(1, 0)
+        addx(1, 0)
         rstd(1, 2)
-        store(1, 1)
+        nmu(1, 1)
+        var(1, 1)
+        nmu(1, 0)
+        rstd(1, 1)
+        dbeta(0, 3)
+        store(0, 2)
+        store(0, 3)
+        cgam(1, 1)
+        cgam(1, 2)
         dV(1, 2)
+        dbeta(0, 0)
+        cgam(1, 0)
+        srs(1, 1)
+        var(1, 0)
+        res(1, 3)
+        s2(1, 3)
+        rstd(1, 0)
+        addx(1, 3)
+        nmu(1, 3)
+        srs(1, 0)
+        cgam(1, 3)
+        var(1, 3)
+        rstd(1, 3)
+        dbeta(1, 1)
+        store(0, 0)
+        dbeta(1, 0)
         store(1, 2)
+        dV(1, 3)
+        store(1, 1)
+        store(1, 0)
+        store(1, 3)

@@ -36,10 +36,12 @@ def tile_linearattentionlayer_pb_kernel(tc, q_feat, kv, k_sum, audio, wo_bytes, 
             nc.sync.dma_start(out=t_[:], in_=q_feat[b, 256 * h : 256 * (h + 1), :].rearrange("(n p) k -> p n k", p=P))
             q_raw[b, h] = t_
 
-        def load_kv(b, g, c):
+        def load_kv(b, g, c, parts=1):
             src = kv[b].rearrange("(g p j) e -> g p j e", p=P, j=4)[g]
             t_ = work.tile([P, 4, 512], BF16, name="kv_raw", bufs=5)
-            nc.sync.dma_start(out=t_[:], in_=src[:, :, 512 * c : 512 * (c + 1)])
+            w = 512 // parts
+            for i in range(parts):
+                nc.sync.dma_start(out=t_[:, :, w * i : w * (i + 1)], in_=src[:, :, 512 * c + w * i : 512 * c + w * (i + 1)])
             kv_raw[b, g, c] = t_
 
         def load_wo(h):
@@ -48,28 +50,29 @@ def tile_linearattentionlayer_pb_kernel(tc, q_feat, kv, k_sum, audio, wo_bytes, 
             wo8[h] = t_
 
         def load_audio(b, n):
-            t_ = work.tile([P, D], BF16, name="au", bufs=4)
+            t_ = work.tile([P, D], BF16, name="au", bufs=6)
             nc.sync.dma_start(out=t_[:], in_=audio[b, P * n : P * (n + 1), :])
             au_raw[b, n] = t_
 
         scol = const.tile([P, 8], F32, name="scol")
-        vec = const.tile([P, D], BF16, name="vec")
+        vec = const.tile([P, P], BF16, name="vec")
+        vcol = const.tile([P, 24], BF16, name="vcol")
         id_f = const.tile([P, P], F32, name="id_f")
         id_b = const.tile([P, P], BF16, name="id_b")
         ks_b = const.tile([P, 16], BF16, name="ks_b")
         nc.vector.memset(vec[:], 0.0)
         make_identity(nc, id_f[:])
         make_identity(nc, id_b[:])
-        nc.sync.dma_start(out=scol[:], in_=wo_scale.rearrange("o (m p) -> p (o m)", p=P))
         load_kv(0, 0, 0)
-        nc.sync.dma_start(out=ks_b[:].rearrange("p (b g t) -> p b g t", b=2, g=2), in_=k_sum.rearrange("b (g p t) -> p b g t", p=P, t=4))
         load_q(0, 0)
-        load_q(0, 1)
-        load_kv(0, 1, 0)
+        nc.sync.dma_start(out=ks_b[:].rearrange("p (b g t) -> p b g t", b=2, g=2), in_=k_sum.rearrange("b (g p t) -> p b g t", p=P, t=4))
+        nc.sync.dma_start(out=scol[:].rearrange("p (g t) -> p g t", g=2), in_=wo_scale.rearrange("o (g p t) -> p (o g) t", p=P, t=4))
         load_kv(0, 0, 1)
+        load_q(0, 1)
         load_wo(0)
+        load_kv(0, 1, 0)
         for i, v in enumerate((bo, gamma, beta)):
-            nc.sync.dma_start(out=vec[i : i + 1, :], in_=v.unsqueeze(0))
+            nc.sync.dma_start(out=vec[8 * i : 8 * (i + 1), :], in_=v.rearrange("(m n) -> m n", n=P))
         load_kv(0, 1, 1)
         load_wo(1)
         load_q(1, 0)
@@ -90,7 +93,7 @@ def tile_linearattentionlayer_pb_kernel(tc, q_feat, kv, k_sum, audio, wo_bytes, 
             gq[b] = const.tile([P, 4096], BF16, name="gq%d" % b, align_bytes=64)
 
         def tqP(b, h, g):
-            xt = psum.tile([P, 2, 2, P], F32, name="tp", tag="bank", bufs=7)
+            xt = psum.tile([P, 2, 2, P], F32, name="tp", tag="bank", bufs=6)
             xq[b, h, g] = xt
             for n in range(2):
                 w = words(q_raw[b, h][:, n, :])
@@ -101,6 +104,11 @@ def tile_linearattentionlayer_pb_kernel(tc, q_feat, kv, k_sum, audio, wo_bytes, 
             o = 2048 * h + 1024 * g
             dst = words(gq[b][:, o : o + 1024]).rearrange("p (n r u) -> p n r u", n=2, u=2)
             nc.scalar.copy(out=dst, in_=xq[b, h, g][:].rearrange("p n u r -> p n r u"))
+
+        def tqV(b, h, g):
+            o = 2048 * h + 1024 * g
+            dst = words(gq[b][:, o : o + 1024]).rearrange("p (n r u) -> p n r u", n=2, u=2)
+            nc.vector.tensor_copy(out=dst, in_=xq[b, h, g][:].rearrange("p n u r -> p n r u"))
 
         def qq(b, h):
             qc[b, h] = work.tile([P, 512], U32, name="qc", bufs=4, align_bytes=64)
@@ -114,20 +122,23 @@ def tile_linearattentionlayer_pb_kernel(tc, q_feat, kv, k_sum, audio, wo_bytes, 
                 grp[b, c] = work.tile([P, 4096], BF16, name="kvg", bufs=2, align_bytes=64)
             return grp[b, c][:, 2048 * g : 2048 * (g + 1)]
 
-        def kvV(b, g, c):
+        def kvD(b, g, c, k):
             dst = kv_dst(b, g, c).rearrange("p (t m j) -> p t m j", t=4, j=4)
-            nc.vector.tensor_copy(out=dst, in_=kv_raw[b, g, c][:].rearrange("p j (m t) -> p t m j", t=4))
+            src = kv_raw[b, g, c][:].rearrange("p j (m t) -> p t m j", t=4)
+            nc.vector.tensor_copy(out=dst[:, 2 * k : 2 * k + 2], in_=src[:, 2 * k : 2 * k + 2])
 
-        def kvS(b, g, c):
+        def kvS(b, g, c, k):
             dst = kv_dst(b, g, c).rearrange("p (t m j) -> p t m j", t=4, j=4)
-            nc.scalar.copy(out=dst, in_=kv_raw[b, g, c][:].rearrange("p j (m t) -> p t m j", t=4))
+            src = kv_raw[b, g, c][:].rearrange("p j (m t) -> p t m j", t=4)
+            nc.scalar.copy(out=dst[:, 2 * k : 2 * k + 2], in_=src[:, 2 * k : 2 * k + 2])
 
         def kvP(b, g, c, k):
-            ib = psum.tile([P, D], BF16, name="ib", tag="bank", bufs=7)
+            if (b, g, c, k) not in ibs:
+                ibs[b, g, c, k] = psum.tile([P, D], BF16, name="ib", tag="bank", bufs=6)
+            ib = ibs[b, g, c, k]
             src = kv_raw[b, g, c][:].rearrange("p j (m t) -> p t m j", t=4)
             for t in range(2):
                 nc.tensor.matmul(ib[:, 512 * t : 512 * (t + 1)], id_b[:], src[:, 2 * k + t], start=True, stop=True)
-            ibs[b, g, c, k] = ib
 
         def kvE(b, g, c, k):
             nc.scalar.copy(out=kv_dst(b, g, c)[:, 1024 * k : 1024 * (k + 1)], in_=ibs[b, g, c, k][:])
@@ -142,21 +153,25 @@ def tile_linearattentionlayer_pb_kernel(tc, q_feat, kv, k_sum, audio, wo_bytes, 
 
         rr = {}
 
-        def ars(b, G, t):
-            if b not in rr:
-                rr[b] = work.tile([P, 8, 512], F32, name="rr", bufs=2)
+        def arsH(b, G, t, h):
+            if (b, h) not in rr:
+                rr[b, h] = work.tile([P, 8, 256], F32, name="rr", bufs=3)
             v = gq[b][:].rearrange("p (h g n j) -> p h g n j", h=2, g=2, j=4)
             i = 4 * G + t
-            nc.scalar.activation(out=rr[b][:, i, :].rearrange("p (h n) -> p h n", h=2), in_=v[:, :, G, :, t], func=ACT.Abs_reciprocal_sqrt, bias=eps[:, 0:1], scale=ks_f[:, 8 * b + i : 8 * b + i + 1])
+            nc.scalar.activation(out=rr[b, h][:, i, :], in_=v[:, h, G, :, t], func=ACT.Abs_reciprocal_sqrt, bias=eps[:, 0:1], scale=ks_f[:, 8 * b + i : 8 * b + i + 1])
 
         def sq(b, h):
-            r = rr[b][:, :, 256 * h : 256 * (h + 1)]
+            r = rr[b, h][:]
             nc.scalar.activation(out=r, in_=r, func=ACT.Square)
+
+        def sqV(b, h):
+            r = rr[b, h][:]
+            nc.vector.tensor_tensor(out=r, in0=r, in1=r, op=ALU.mult)
 
         at, ac, acs, num = {}, {}, {}, {}
 
         def s1(b, n, G):
-            num[b, n, G] = psum.tile([P, 4, P], F32, name="num", tag="bank", bufs=7)
+            num[b, n, G] = psum.tile([P, 4, P], F32, name="num", tag="bank", bufs=6)
             for t in range(4):
                 for g in range(2):
                     cs = slice(512 * g + P * t, 512 * g + P * (t + 1))
@@ -164,61 +179,78 @@ def tile_linearattentionlayer_pb_kernel(tc, q_feat, kv, k_sum, audio, wo_bytes, 
                     nc.tensor.matmul_mx(out=num[b, n, G][:, t, :], lhsT=kc[b, G][:, cs].bitcast(FP8X4), lhsT_scale=kss[b, G][:, cs], rhs=qc[b, n // 2][:, o : o + P].bitcast(FP8X4), rhs_scale=qs[b, n // 2][:, o : o + P], start=(g == 0), stop=(g == 1))
 
         def mul(b, n, G):
-            ns = slice(P * n, P * (n + 1))
+            ns = slice(P * (n % 2), P * (n % 2 + 1))
             if (b, n // 2) not in at:
                 at[b, n // 2] = work.tile([P, 2048], BF16, name="at", bufs=2, align_bytes=64)
             o = 1024 * G + 512 * (n % 2)
-            nc.vector.tensor_tensor(out=at[b, n // 2][:, o : o + 512].rearrange("p (n j) -> p n j", j=4), in0=num[b, n, G][:].rearrange("p j n -> p n j"), in1=rr[b][:, 4 * G : 4 * (G + 1), ns].rearrange("p j n -> p n j"), op=ALU.mult)
+            nc.vector.tensor_tensor(out=at[b, n // 2][:, o : o + 512].rearrange("p (n j) -> p n j", j=4), in0=num[b, n, G][:].rearrange("p j n -> p n j"), in1=rr[b, n // 2][:, 4 * G : 4 * (G + 1), ns].rearrange("p j n -> p n j"), op=ALU.mult)
 
         def aq(b, h):
             ac[b, h] = work.tile([P, 512], U32, name="ac", bufs=4, align_bytes=64)
             acs[b, h] = work.tile([P, 512], U8, name="acs", bufs=4, align_bytes=64)
             nc.vector.quantize_mx(out=ac[b, h][:].bitcast(FP8X4), scales=acs[b, h][:], in_=at[b, h][:])
 
-        sc_bc = const.tile([P, D], F32, name="sc_bc")
-        bo_bc = const.tile([P, D], BF16, name="bo_bc")
-        be_bc = const.tile([P, D], BF16, name="be_bc")
         gam = psum.tile([P, D], BF16, name="gam", bufs=1)
+        bet = psum.tile([P, D], BF16, name="bet", bufs=1)
         spr = {}
 
-        def spsP(h):
-            spr[h] = psum.tile([P, 512], F32, name="sp", tag="bank", bufs=7)
-            for m in range(4):
-                nc.tensor.matmul(spr[h][:, P * m : P * (m + 1)], scol[:, 4 * h + m : 4 * h + m + 1].to_broadcast([P, P]), id_f[:], start=True, stop=True)
+        bo_bc = const.tile([P, D], BF16, name="bo_bc")
+        be_bc = const.tile([P, D], BF16, name="be_bc")
+        gam_bc = const.tile([P, D], BF16, name="gam_bc")
 
-        def spsS(h):
-            nc.scalar.copy(out=sc_bc[:, 512 * h : 512 * (h + 1)], in_=spr[h][:])
+        def vecP():
+            spr["t"] = psum.tile([P, P], BF16, name="vt", tag="bank", bufs=6)
+            nc.tensor.transpose(spr["t"][:], vec[:], id_b[:])
 
-        def spread_row(i, dst):
-            vb = gam if i == 1 else psum.tile([P, D], BF16, name="vb", tag="bank", bufs=7)
-            for h in range(2):
-                hs = slice(512 * h, 512 * (h + 1))
-                nc.tensor.matmul(vb[:, hs], id_b[:, i : i + 1].to_broadcast([P, P]), vec[:, hs], start=True, stop=True)
+        def vecS():
+            nc.scalar.copy(out=vcol[:], in_=spr["t"][:, 0:24])
+
+        def spread(i):
+            vb = (None, gam, bet)[i] if i else psum.tile([P, D], BF16, name="vb", tag="bank", bufs=6)
+            for m in range(8):
+                nc.tensor.transpose(vb[:, P * m : P * (m + 1)], vcol[:, 8 * i + m : 8 * i + m + 1].to_broadcast([P, P]), id_b[:])
             spr["v", i] = vb
 
-        def sprS(i, dst):
-            nc.scalar.copy(out=dst[:], in_=spr["v", i][:])
+        def spreadV(i):
+            nc.vector.tensor_copy(out=(bo_bc, gam_bc, be_bc)[i][:], in_=spr["v", i][:])
+
+        def spreadS(i):
+            nc.scalar.copy(out=(bo_bc, gam_bc, be_bc)[i][:], in_=spr["v", i][:])
 
         wc, wsc, gw, wb = {}, {}, {}, {}
 
-        def wo(r):
-            wb[r] = work.tile([P, D], BF16, name="wb", bufs=4)
-            nc.vector.tensor_tensor(out=wb[r][:], in0=wo8[r // 4][:, r % 4, :].bitcast(FP8), in1=sc_bc[:], op=ALU.mult)
+        def wb_tile(r):
+            if r not in wb:
+                wb[r] = work.tile([P, D], BF16, name="wb", bufs=4)
+            return wb[r][:], wo8[r // 4][:, r % 4, :].bitcast(FP8)
+
+        def castG(r):
+            o, i = wb_tile(r)
+            nc.gpsimd.tensor_copy(out=o, in_=i)
+
+        def castV(r):
+            o, i = wb_tile(r)
+            nc.vector.tensor_copy(out=o, in_=i)
+
+        def castS(r):
+            o, i = wb_tile(r)
+            nc.scalar.copy(out=o, in_=i)
 
         def twP(rp, G):
-            xt = psum.tile([P, 2, 2, P], F32, name="tp", tag="bank", bufs=7)
+            xt = psum.tile([P, 2, 2, P], F32, name="tp", tag="bank", bufs=6)
             xq[rp, G] = xt
             for k in range(2):
                 for u in range(2):
-                    nc.tensor.transpose(xt[:, k, u, :], words(wb[2 * rp + k][:])[:, 256 * G + u : 256 * (G + 1) : 2], id_f[:])
+                    nc.tensor.transpose(xt[:, u, k, :], words(wb[2 * rp + k][:])[:, 256 * G + u : 256 * (G + 1) : 2], id_f[:])
 
-        def twS(rp, G):
+        def twM(rp, G):
             h, i = rp // 2, rp % 2
             if h not in gw:
                 gw[h] = work.tile([P, 4096], BF16, name="gw", bufs=1, align_bytes=64)
             o = 2048 * G + 1024 * i
-            dst = words(gw[h][:, o : o + 1024]).rearrange("p (n r u) -> p n r u", n=2, u=2)
-            nc.scalar.copy(out=dst, in_=xq[rp, G][:].rearrange("p n u r -> p n r u"))
+            sc = scol[:, 4 * G : 4 * G + 4].rearrange("p (u v) -> p u v", u=2).unsqueeze(1).to_broadcast([P, 2 * P, 2, 2])
+            src = xq[rp, G][:].rearrange("p u k r -> p (u k r)").bitcast(BF16).rearrange("p (u f v) -> p f u v", u=2, v=2)
+            nc.vector.tensor_tensor(out=gw[h][:, o : o + 1024].rearrange("p (f u v) -> p f u v", u=2, v=2), in0=src, in1=sc, op=ALU.mult)
 
         def wq(h):
             wc[h] = const.tile([P, D], U32, name="wc%d" % h, align_bytes=64)
@@ -228,13 +260,13 @@ def tile_linearattentionlayer_pb_kernel(tc, q_feat, kv, k_sum, audio, wo_bytes, 
         aa = {}
 
         def res(b, n):
-            aa[b, n] = work.tile([P, D], F32, name="aa", bufs=3)
-            for h in range(2):
-                hs = slice(512 * h, 512 * (h + 1))
-                nc.gpsimd.tensor_tensor(out=aa[b, n][:, hs], in0=au_raw[b, n][:, hs], in1=bo_bc[:, hs], op=ALU.add)
+            if (b, n) not in aa:
+                aa[b, n] = work.tile([P, D], F32, name="aa", bufs=4)
+            nc.gpsimd.tensor_tensor(out=aa[b, n][:], in0=au_raw[b, n][:], in1=bo_bc[:], op=ALU.add)
 
         def resV(b, n):
-            aa[b, n] = work.tile([P, D], F32, name="aa", bufs=3)
+            if (b, n) not in aa:
+                aa[b, n] = work.tile([P, D], F32, name="aa", bufs=4)
             nc.vector.tensor_tensor(out=aa[b, n][:], in0=au_raw[b, n][:], in1=bo_bc[:], op=ALU.add)
 
         y, x, xn, st, sv = {}, {}, {}, {}, {}
@@ -242,7 +274,7 @@ def tile_linearattentionlayer_pb_kernel(tc, q_feat, kv, k_sum, audio, wo_bytes, 
         def s2(b, n):
             o = P * (n % 2)
             for h in range(2):
-                y[b, n, h] = psum.tile([P, 512], F32, name="y", tag="bank", bufs=7)
+                y[b, n, h] = psum.tile([P, 512], F32, name="y", tag="bank", bufs=6)
                 for G in range(2):
                     ts = slice(256 * G + o, 256 * G + o + P)
                     ws = slice(512 * G, 512 * (G + 1))
@@ -258,6 +290,9 @@ def tile_linearattentionlayer_pb_kernel(tc, q_feat, kv, k_sum, audio, wo_bytes, 
         def nmu(b, n):
             nc.vector.tensor_scalar(out=st[b, n][:, 2:3], in0=st[b, n][:, 0:1], scalar1=st[b, n][:, 1:2], scalar2=-1.0 / D, op0=ALU.add, op1=ALU.mult)
 
+        def nmuS(b, n):
+            nc.scalar.activation(out=st[b, n][:, 3:5], in_=st[b, n][:, 0:2], func=ACT.Copy, scale=-1.0 / D, accum_out=st[b, n][:, 2:3])
+
         def var(b, n):
             sv[b, n] = work.tile([P, 8], F32, name="sv", bufs=4)
             junk = work.tile([P, D], BF16, name="junk", bufs=1)
@@ -267,233 +302,282 @@ def tile_linearattentionlayer_pb_kernel(tc, q_feat, kv, k_sum, audio, wo_bytes, 
             nc.scalar.activation(out=sv[b, n][:, 1:2], in_=sv[b, n][:, 0:1], func=ACT.Abs_reciprocal_sqrt, bias=eps[:, 1:2], scale=1.0 / D)
 
         def cgam(b, n):
-            xn[b, n] = work.tile([P, D], F32, name="xn", bufs=3)
+            if (b, n) not in xn:
+                xn[b, n] = work.tile([P, D], F32, name="xn", bufs=4)
             nc.vector.scalar_tensor_tensor(out=xn[b, n][:], in0=x[b, n][:], scalar=st[b, n][:, 2:3], in1=gam[:], op0=ALU.add, op1=ALU.mult)
 
         def srs(b, n):
             nc.scalar.activation(out=xn[b, n][:], in_=xn[b, n][:], func=ACT.Copy, scale=sv[b, n][:, 1:2])
 
         def dbeta(b, n):
-            for h in range(2):
-                hs = slice(512 * h, 512 * (h + 1))
-                nc.gpsimd.tensor_tensor(out=xn[b, n][:, hs], in0=xn[b, n][:, hs], in1=be_bc[:, hs], op=ALU.add)
+            nc.gpsimd.tensor_tensor(out=xn[b, n][:], in0=xn[b, n][:], in1=be_bc[:], op=ALU.add)
 
         def dV(b, n):
-            nc.vector.scalar_tensor_tensor(out=xn[b, n][:], in0=xn[b, n][:], scalar=sv[b, n][:, 1:2], in1=be_bc[:], op0=ALU.mult, op1=ALU.add)
+            nc.vector.scalar_tensor_tensor(out=xn[b, n][:], in0=xn[b, n][:], scalar=sv[b, n][:, 1:2], in1=bet[:], op0=ALU.mult, op1=ALU.add)
+
+        def dVh(b, n, h):
+            hs = slice(512 * h, 512 * (h + 1))
+            nc.vector.scalar_tensor_tensor(out=xn[b, n][:, hs], in0=xn[b, n][:, hs], scalar=sv[b, n][:, 1:2], in1=bet[:, hs], op0=ALU.mult, op1=ALU.add)
+
+        def storeh(b, n, h):
+            hs = slice(512 * h, 512 * (h + 1))
+            nc.sync.dma_start(out=out[b, P * n : P * (n + 1), hs], in_=xn[b, n][:, hs])
+
+        def nmr(b, n):
+            nc.scalar.activation(out=sv[b, n][:, 2:3], in_=st[b, n][:, 2:3], func=ACT.Copy, scale=sv[b, n][:, 1:2])
+
+        def normS(b, n):
+            if (b, n) not in xn:
+                xn[b, n] = work.tile([P, D], F32, name="xn", bufs=4)
+            nc.scalar.activation(out=xn[b, n][:], in_=x[b, n][:], func=ACT.Identity, scale=sv[b, n][:, 1:2], bias=sv[b, n][:, 2:3])
+
+        def normV(b, n):
+            if (b, n) not in xn:
+                xn[b, n] = work.tile([P, D], F32, name="xn", bufs=4)
+            nc.vector.tensor_scalar(out=xn[b, n][:], in0=x[b, n][:], scalar1=st[b, n][:, 2:3], scalar2=sv[b, n][:, 1:2], op0=ALU.add, op1=ALU.mult)
+
+        def gG(b, n):
+            nc.gpsimd.tensor_tensor(out=xn[b, n][:], in0=xn[b, n][:], in1=gam_bc[:], op=ALU.mult)
 
         def store(b, n):
             nc.sync.dma_start(out=out[b, P * n : P * (n + 1), :], in_=xn[b, n][:])
 
-        kvV(0, 0, 0)
-        spsP(0)
-        spsS(0)
+        kvP(0, 0, 0, 1)
+        kvD(0, 0, 0, 0)
+        kvD(0, 0, 1, 0)
         tqP(0, 0, 1)
+        kvE(0, 0, 0, 1)
         tqP(0, 0, 0)
-        spsP(1)
         tqS(0, 0, 1)
+        kvP(0, 0, 1, 1)
+        castV(0)
+        castV(1)
         tqP(0, 1, 1)
-        tqS(0, 0, 0)
-        spsS(1)
         tqP(0, 1, 0)
-        tqS(0, 1, 1)
+        vecP()
+        tqS(0, 0, 0)
+        castS(3)
+        castS(2)
+        vecS()
         tqS(0, 1, 0)
-        kvP(0, 1, 0, 0)
-        kvP(0, 1, 0, 1)
-        qq(0, 0)
-        kvV(0, 0, 1)
-        kvP(0, 1, 1, 0)
-        ars(0, 0, 0)
-        wo(0)
-        ars(0, 0, 2)
-        wo(1)
-        ars(0, 0, 3)
-        ars(0, 1, 0)
-        ars(0, 0, 1)
-        ars(0, 1, 2)
-        ars(0, 1, 1)
+        tqS(0, 1, 1)
+        kvE(0, 0, 1, 1)
         twP(0, 1)
+        arsH(0, 1, 1, 1)
+        arsH(0, 1, 3, 0)
+        arsH(0, 0, 0, 1)
         twP(0, 0)
-        kvP(0, 1, 1, 1)
-        twS(0, 0)
-        kvE(0, 1, 0, 1)
-        wo(3)
-        wo(2)
-        kvE(0, 1, 0, 0)
-        tqP(1, 0, 1)
-        kvE(0, 1, 1, 0)
+        arsH(0, 0, 1, 0)
+        kvD(0, 1, 0, 1)
+        kvP(0, 1, 0, 0)
+        qq(0, 0)
+        arsH(0, 0, 3, 1)
+        arsH(0, 1, 0, 1)
+        arsH(0, 0, 0, 0)
         twP(1, 1)
-        kvE(0, 1, 1, 1)
-        wo(7)
-        twS(0, 1)
-        tqP(1, 1, 1)
+        arsH(0, 1, 2, 1)
         twP(1, 0)
-        wo(4)
-        tqP(1, 0, 0)
-        tqS(1, 1, 1)
-        tqP(1, 1, 0)
-        kq(0, 1)
-        ars(0, 1, 3)
-        wo(6)
-        spread_row(0, bo_bc)
-        twP(3, 0)
-        twS(1, 1)
-        tqS(1, 1, 0)
-        kvP(1, 1, 0, 0)
-        tqS(1, 0, 0)
-        qq(0, 1)
-        kvP(1, 1, 0, 1)
-        twP(3, 1)
+        kvP(0, 1, 1, 1)
+        arsH(0, 0, 3, 0)
+        tqP(1, 0, 1)
+        kvD(0, 1, 1, 0)
+        spread(0)
+        arsH(0, 1, 2, 0)
+        kvP(1, 0, 0, 0)
+        twM(0, 0)
+        twM(0, 1)
+        arsH(0, 0, 2, 0)
         tqS(1, 0, 1)
-        s1(0, 1, 1)
-        twS(1, 0)
-        sprS(0, bo_bc)
-        kq(0, 0)
-        kvP(1, 1, 1, 0)
-        s1(0, 1, 0)
-        kvV(1, 0, 0)
-        resV(0, 1)
-        ars(1, 1, 0)
-        kvE(1, 1, 0, 1)
-        qq(1, 1)
-        ars(1, 0, 0)
-        kvE(1, 1, 0, 0)
-        s1(0, 0, 0)
-        qq(1, 0)
-        ars(1, 0, 1)
-        s1(0, 2, 0)
-        sq(0, 0)
+        kvE(0, 1, 1, 1)
+        castG(6)
+        twM(1, 1)
+        castG(7)
+        kvE(0, 1, 0, 0)
+        tqP(1, 0, 0)
+        twM(1, 0)
         wq(0)
-        wo(5)
-        resV(0, 0)
-        s1(0, 0, 1)
-        mul(0, 1, 1)
-        ars(1, 1, 3)
-        kvE(1, 1, 1, 0)
-        twS(3, 1)
-        sq(0, 1)
-        ars(1, 0, 2)
-        twS(3, 0)
-        kq(1, 0)
-        ars(1, 1, 2)
-        kvV(1, 0, 1)
-        s1(0, 2, 1)
-        res(1, 1)
-        kvP(1, 1, 1, 1)
-        mul(0, 2, 1)
-        spread_row(2, be_bc)
-        kvE(1, 1, 1, 1)
-        mul(0, 1, 0)
+        tqS(1, 0, 0)
+        castG(4)
+        castG(5)
+        arsH(0, 0, 2, 1)
+        twP(3, 0)
+        arsH(0, 1, 0, 0)
+        arsH(0, 0, 1, 1)
+        kvP(1, 1, 1, 0)
+        kq(0, 1)
+        spreadS(0)
+        tqP(1, 1, 0)
+        tqS(1, 1, 0)
         twP(2, 1)
+        qq(0, 1)
+        kvE(1, 1, 1, 0)
+        kvP(1, 1, 0, 1)
+        kvE(1, 0, 0, 0)
+        qq(1, 0)
+        arsH(0, 1, 3, 1)
+        arsH(0, 1, 1, 0)
+        twP(3, 1)
+        kq(0, 0)
+        kvE(1, 1, 0, 1)
+        sq(0, 1)
         twP(2, 0)
+        arsH(1, 1, 2, 0)
+        s1(0, 2, 1)
         s1(0, 3, 1)
-        twS(2, 1)
-        twS(2, 0)
-        mul(0, 0, 1)
-        mul(0, 0, 0)
+        sq(0, 0)
+        arsH(1, 1, 0, 0)
+        s1(0, 3, 0)
+        s1(0, 2, 0)
+        res(0, 3)
+        arsH(1, 0, 0, 0)
+        twM(2, 1)
+        twM(3, 0)
+        s1(0, 0, 1)
+        twM(2, 0)
+        arsH(1, 0, 2, 0)
+        twM(3, 1)
         mul(0, 2, 0)
+        mul(0, 2, 1)
+        mul(0, 3, 1)
+        s1(0, 1, 0)
+        arsH(1, 1, 3, 0)
+        arsH(1, 0, 0, 1)
+        s1(0, 1, 1)
+        arsH(1, 0, 3, 0)
+        s1(0, 0, 0)
+        kvP(1, 1, 0, 0)
+        mul(0, 3, 0)
+        mul(0, 0, 0)
+        kvP(1, 0, 1, 1)
+        tqP(1, 1, 1)
+        arsH(1, 0, 2, 1)
+        kvP(1, 0, 0, 1)
+        res(0, 2)
+        arsH(1, 0, 1, 0)
+        tqS(1, 1, 1)
+        arsH(1, 1, 1, 0)
+        kvP(1, 0, 1, 0)
+        kvE(1, 1, 0, 0)
+        kvE(1, 0, 0, 1)
+        mul(0, 0, 1)
+        arsH(1, 0, 3, 1)
+        mul(0, 1, 1)
+        kvP(1, 1, 1, 1)
+        mul(0, 1, 0)
+        aq(0, 1)
         aq(0, 0)
         wq(1)
-        spread_row(1, None)
-        s2(0, 1)
-        kq(1, 1)
-        sprS(2, be_bc)
-        ars(1, 1, 1)
-        addx(0, 1)
         s2(0, 0)
-        s1(1, 1, 1)
-        ars(1, 0, 3)
-        sq(1, 1)
-        s1(0, 3, 0)
-        res(0, 2)
-        sq(1, 0)
-        mul(0, 3, 1)
-        s1(1, 3, 0)
-        res(0, 3)
-        nmu(0, 1)
-        mul(0, 3, 0)
-        s1(1, 3, 1)
-        var(0, 1)
+        kq(1, 0)
+        s2(0, 1)
+        qq(1, 1)
         s1(1, 0, 0)
-        addx(0, 0)
-        rstd(0, 1)
-        aq(0, 1)
-        cgam(0, 1)
-        s2(0, 2)
-        addx(0, 2)
-        srs(0, 1)
-        s1(1, 2, 1)
-        mul(1, 0, 0)
-        nmu(0, 2)
-        s1(1, 2, 0)
-        s1(1, 1, 0)
         s2(0, 3)
-        mul(1, 3, 0)
-        s1(1, 0, 1)
-        mul(1, 3, 1)
+        kvE(1, 0, 1, 1)
+        arsH(1, 1, 1, 1)
+        kvE(1, 1, 1, 1)
+        res(0, 1)
+        res(0, 0)
+        kvE(1, 0, 1, 0)
+        arsH(1, 0, 1, 1)
+        addx(0, 0)
+        kq(1, 1)
+        s1(1, 1, 1)
         addx(0, 3)
-        var(0, 2)
-        dbeta(0, 1)
-        store(0, 1)
-        mul(1, 2, 0)
-        res(1, 2)
-        mul(1, 2, 1)
-        rstd(0, 2)
-        nmu(0, 3)
-        var(0, 3)
-        cgam(0, 2)
+        sq(1, 0)
+        s1(1, 1, 0)
+        nmuS(0, 0)
+        spread(1)
         mul(1, 1, 1)
-        mul(1, 0, 1)
-        mul(1, 1, 0)
-        srs(0, 2)
-        nmu(0, 0)
-        cgam(0, 3)
-        rstd(0, 3)
-        aq(1, 1)
-        cgam(0, 0)
-        aq(1, 0)
-        s2(1, 2)
-        s2(1, 1)
-        addx(1, 2)
-        nmu(1, 2)
+        arsH(1, 1, 3, 1)
         var(0, 0)
-        res(1, 0)
-        srs(0, 3)
-        addx(1, 1)
-        dbeta(0, 2)
+        res(1, 2)
+        nmuS(0, 3)
         rstd(0, 0)
-        srs(0, 0)
-        var(1, 2)
+        s2(0, 2)
+        mul(1, 0, 0)
+        s1(1, 0, 1)
+        spread(2)
+        s1(1, 2, 1)
+        spreadS(1)
+        addx(0, 1)
+        mul(1, 0, 1)
+        s1(1, 2, 0)
+        mul(1, 1, 0)
+        nmr(0, 0)
+        res(1, 0)
+        s1(1, 3, 0)
+        nmu(0, 1)
+        cgam(0, 1)
+        aq(1, 0)
+        normS(0, 0)
         s2(1, 0)
+        arsH(1, 1, 0, 1)
+        var(0, 3)
+        arsH(1, 1, 2, 1)
+        rstd(0, 3)
+        s1(1, 3, 1)
+        sq(1, 1)
+        spreadS(2)
+        addx(0, 2)
+        mul(1, 2, 1)
+        nmuS(0, 2)
+        cgam(0, 3)
+        gG(0, 0)
+        var(0, 1)
+        rstd(0, 1)
+        s2(1, 1)
         addx(1, 0)
-        rstd(1, 2)
-        nmu(1, 1)
-        var(1, 1)
-        nmu(1, 0)
-        rstd(1, 1)
-        dbeta(0, 3)
-        store(0, 2)
-        store(0, 3)
-        cgam(1, 1)
-        cgam(1, 2)
-        dV(1, 2)
-        dbeta(0, 0)
-        cgam(1, 0)
-        srs(1, 1)
-        var(1, 0)
+        mul(1, 2, 0)
+        var(0, 2)
         res(1, 3)
-        s2(1, 3)
+        nmuS(1, 0)
+        mul(1, 3, 0)
+        mul(1, 3, 1)
+        var(1, 0)
+        aq(1, 1)
+        srs(0, 1)
         rstd(1, 0)
+        cgam(0, 2)
+        dbeta(0, 0)
+        nmr(1, 0)
+        s2(1, 3)
+        dV(0, 3)
+        s2(1, 2)
+        rstd(0, 2)
+        normS(1, 0)
+        srs(0, 2)
+        addx(1, 2)
+        nmuS(1, 2)
+        res(1, 1)
+        addx(1, 1)
+        var(1, 2)
         addx(1, 3)
-        nmu(1, 3)
-        srs(1, 0)
-        cgam(1, 3)
-        var(1, 3)
-        rstd(1, 3)
-        dbeta(1, 1)
+        cgam(1, 2)
+        nmuS(1, 1)
+        var(1, 1)
         store(0, 0)
+        nmuS(1, 3)
+        rstd(1, 1)
+        dbeta(0, 1)
+        rstd(1, 2)
+        srs(1, 2)
+        var(1, 3)
+        store(0, 1)
+        gG(1, 0)
+        cgam(1, 1)
+        store(0, 3)
+        dbeta(0, 2)
         dbeta(1, 0)
-        store(1, 2)
-        dV(1, 3)
-        store(1, 1)
+        rstd(1, 3)
+        store(0, 2)
+        dV(1, 1)
         store(1, 0)
-        store(1, 3)
+        cgam(1, 3)
+        dVh(1, 3, 0)
+        store(1, 1)
+        dbeta(1, 2)
+        store(1, 2)
+        storeh(1, 3, 0)
+        dVh(1, 3, 1)
+        storeh(1, 3, 1)

@@ -29,16 +29,25 @@ def tile_linearattentionlayer_pb_kernel(tc, q_feat, kv, k_sum, audio, wo_bytes, 
         psum = ctx.enter_context(tc.psum_pool(name="psum", bufs=1))
         ctx.enter_context(tc.manual_schedule())
 
+        count = {}
+
+        def rot(pool, shape, dtype, name, n, align_bytes=None):
+            i = count.setdefault(name, 0)
+            count[name] = i + 1
+            if align_bytes is None:
+                return pool.tile(shape, dtype, name=name, tag="%s_%d_%d" % (name, i % n, n), bufs=1)
+            return pool.tile(shape, dtype, name=name, tag="%s_%d_%d" % (name, i % n, n), bufs=1, align_bytes=align_bytes)
+
         q_raw, kv_raw, au_raw, wo8 = {}, {}, {}, {}
 
         def load_q(b, h):
-            t_ = work.tile([P, 2, D], BF16, name="q_raw", bufs=3)
+            t_ = rot(work, [P, 2, D], BF16, "q_raw", 3)
             nc.sync.dma_start(out=t_[:], in_=q_feat[b, 256 * h : 256 * (h + 1), :].rearrange("(n p) k -> p n k", p=P))
             q_raw[b, h] = t_
 
         def load_kv(b, g, c, parts=1):
             src = kv[b].rearrange("(g p j) e -> g p j e", p=P, j=4)[g]
-            t_ = work.tile([P, 4, 512], BF16, name="kv_raw", bufs=5)
+            t_ = rot(work, [P, 4, 512], BF16, "kv_raw", 5)
             w = 512 // parts
             for i in range(parts):
                 nc.sync.dma_start(out=t_[:, :, w * i : w * (i + 1)], in_=src[:, :, 512 * c + w * i : 512 * c + w * (i + 1)])
@@ -50,17 +59,19 @@ def tile_linearattentionlayer_pb_kernel(tc, q_feat, kv, k_sum, audio, wo_bytes, 
             wo8[h] = t_
 
         def load_audio(b, n):
-            t_ = work.tile([P, D], BF16, name="au", bufs=6)
+            t_ = rot(work, [P, D], BF16, "au", 6)
             nc.sync.dma_start(out=t_[:], in_=audio[b, P * n : P * (n + 1), :])
             au_raw[b, n] = t_
 
         scol = const.tile([P, 8], F32, name="scol")
-        vec = const.tile([P, P], BF16, name="vec")
+        vec = {}
+        for i in range(3):
+            vec[i] = const.tile([P, P], BF16, name="vec%d" % i)
+            nc.vector.memset(vec[i][:], 0.0)
         vcol = const.tile([P, 24], BF16, name="vcol")
         id_f = const.tile([P, P], F32, name="id_f")
         id_b = const.tile([P, P], BF16, name="id_b")
         ks_b = const.tile([P, 16], BF16, name="ks_b")
-        nc.vector.memset(vec[:], 0.0)
         make_identity(nc, id_f[:])
         make_identity(nc, id_b[:])
         load_kv(0, 0, 0)
@@ -71,17 +82,22 @@ def tile_linearattentionlayer_pb_kernel(tc, q_feat, kv, k_sum, audio, wo_bytes, 
         load_q(0, 1)
         load_wo(0)
         load_kv(0, 1, 0)
-        for i, v in enumerate((bo, gamma, beta)):
-            nc.sync.dma_start(out=vec[8 * i : 8 * (i + 1), :], in_=v.rearrange("(m n) -> m n", n=P))
         load_kv(0, 1, 1)
         load_wo(1)
         load_q(1, 0)
         load_q(1, 1)
         for g, c in ((0, 0), (1, 0), (0, 1), (1, 1)):
             load_kv(1, g, c)
-        for b in range(2):
-            for n in range(4):
-                load_audio(b, n)
+        def load_vec(i, v):
+            nc.sync.dma_start(out=vec[i][0:8, :], in_=v.rearrange("(m n) -> m n", n=P))
+
+        load_vec(0, bo)
+        for n in range(4):
+            load_audio(0, n)
+        load_vec(1, gamma)
+        load_vec(2, beta)
+        for n in range(4):
+            load_audio(1, n)
         ks_f = const.tile([P, 16], F32, name="ks_f")
         eps = const.tile([P, 2], F32, name="eps")
         nc.gpsimd.tensor_scalar(out=eps[:, 0:1], in0=id_f[:, 0:1], scalar1=0.0, scalar2=1e-6, op0=ALU.mult, op1=ALU.add)
@@ -93,7 +109,7 @@ def tile_linearattentionlayer_pb_kernel(tc, q_feat, kv, k_sum, audio, wo_bytes, 
             gq[b] = const.tile([P, 4096], BF16, name="gq%d" % b, align_bytes=64)
 
         def tqP(b, h, g):
-            xt = psum.tile([P, 2, 2, P], F32, name="tp", tag="bank", bufs=6)
+            xt = rot(psum, [P, 2, 2, P], F32, "bank", 6)
             xq[b, h, g] = xt
             for n in range(2):
                 w = words(q_raw[b, h][:, n, :])
@@ -111,15 +127,15 @@ def tile_linearattentionlayer_pb_kernel(tc, q_feat, kv, k_sum, audio, wo_bytes, 
             nc.vector.tensor_copy(out=dst, in_=xq[b, h, g][:].rearrange("p n u r -> p n r u"))
 
         def qq(b, h):
-            qc[b, h] = work.tile([P, 512], U32, name="qc", bufs=4, align_bytes=64)
-            qs[b, h] = work.tile([P, 512], U8, name="qs", bufs=4, align_bytes=64)
+            qc[b, h] = rot(work, [P, 512], U32, "qc", 4, align_bytes=64)
+            qs[b, h] = rot(work, [P, 512], U8, "qs", 4, align_bytes=64)
             nc.vector.quantize_mx(out=qc[b, h][:].bitcast(FP8X4), scales=qs[b, h][:], in_=gq[b][:, 2048 * h : 2048 * (h + 1)])
 
         kc, kss, grp, ibs = {}, {}, {}, {}
 
         def kv_dst(b, g, c):
             if (b, c) not in grp:
-                grp[b, c] = work.tile([P, 4096], BF16, name="kvg", bufs=2, align_bytes=64)
+                grp[b, c] = rot(work, [P, 4096], BF16, "kvg", 2, align_bytes=64)
             return grp[b, c][:, 2048 * g : 2048 * (g + 1)]
 
         def kvD(b, g, c, k):
@@ -134,7 +150,7 @@ def tile_linearattentionlayer_pb_kernel(tc, q_feat, kv, k_sum, audio, wo_bytes, 
 
         def kvP(b, g, c, k):
             if (b, g, c, k) not in ibs:
-                ibs[b, g, c, k] = psum.tile([P, D], BF16, name="ib", tag="bank", bufs=6)
+                ibs[b, g, c, k] = rot(psum, [P, D], BF16, "bank", 6)
             ib = ibs[b, g, c, k]
             src = kv_raw[b, g, c][:].rearrange("p j (m t) -> p t m j", t=4)
             for t in range(2):
@@ -147,15 +163,15 @@ def tile_linearattentionlayer_pb_kernel(tc, q_feat, kv, k_sum, audio, wo_bytes, 
             nc.vector.tensor_copy(out=kv_dst(b, g, c)[:, 1024 * k : 1024 * (k + 1)], in_=ibs[b, g, c, k][:])
 
         def kq(b, c):
-            kc[b, c] = work.tile([P, D], U32, name="kc", bufs=4, align_bytes=64)
-            kss[b, c] = work.tile([P, D], U8, name="kss", bufs=4, align_bytes=64)
+            kc[b, c] = rot(work, [P, D], U32, "kc", 4, align_bytes=64)
+            kss[b, c] = rot(work, [P, D], U8, "kss", 4, align_bytes=64)
             nc.vector.quantize_mx(out=kc[b, c][:].bitcast(FP8X4), scales=kss[b, c][:], in_=grp[b, c][:])
 
         rr = {}
 
         def arsH(b, G, t, h):
             if (b, h) not in rr:
-                rr[b, h] = work.tile([P, 8, 256], F32, name="rr", bufs=3)
+                rr[b, h] = rot(work, [P, 8, 256], F32, "rr", 3)
             v = gq[b][:].rearrange("p (h g n j) -> p h g n j", h=2, g=2, j=4)
             i = 4 * G + t
             nc.scalar.activation(out=rr[b, h][:, i, :], in_=v[:, h, G, :, t], func=ACT.Abs_reciprocal_sqrt, bias=eps[:, 0:1], scale=ks_f[:, 8 * b + i : 8 * b + i + 1])
@@ -171,7 +187,7 @@ def tile_linearattentionlayer_pb_kernel(tc, q_feat, kv, k_sum, audio, wo_bytes, 
         at, ac, acs, num = {}, {}, {}, {}
 
         def s1(b, n, G):
-            num[b, n, G] = psum.tile([P, 4, P], F32, name="num", tag="bank", bufs=6)
+            num[b, n, G] = rot(psum, [P, 4, P], F32, "bank", 6)
             for t in range(4):
                 for g in range(2):
                     cs = slice(512 * g + P * t, 512 * g + P * (t + 1))
@@ -181,13 +197,13 @@ def tile_linearattentionlayer_pb_kernel(tc, q_feat, kv, k_sum, audio, wo_bytes, 
         def mul(b, n, G):
             ns = slice(P * (n % 2), P * (n % 2 + 1))
             if (b, n // 2) not in at:
-                at[b, n // 2] = work.tile([P, 2048], BF16, name="at", bufs=2, align_bytes=64)
+                at[b, n // 2] = rot(work, [P, 2048], BF16, "at", 2, align_bytes=64)
             o = 1024 * G + 512 * (n % 2)
             nc.vector.tensor_tensor(out=at[b, n // 2][:, o : o + 512].rearrange("p (n j) -> p n j", j=4), in0=num[b, n, G][:].rearrange("p j n -> p n j"), in1=rr[b, n // 2][:, 4 * G : 4 * (G + 1), ns].rearrange("p j n -> p n j"), op=ALU.mult)
 
         def aq(b, h):
-            ac[b, h] = work.tile([P, 512], U32, name="ac", bufs=4, align_bytes=64)
-            acs[b, h] = work.tile([P, 512], U8, name="acs", bufs=4, align_bytes=64)
+            ac[b, h] = rot(work, [P, 512], U32, "ac", 4, align_bytes=64)
+            acs[b, h] = rot(work, [P, 512], U8, "acs", 4, align_bytes=64)
             nc.vector.quantize_mx(out=ac[b, h][:].bitcast(FP8X4), scales=acs[b, h][:], in_=at[b, h][:])
 
         gam = psum.tile([P, D], BF16, name="gam", bufs=1)
@@ -198,15 +214,15 @@ def tile_linearattentionlayer_pb_kernel(tc, q_feat, kv, k_sum, audio, wo_bytes, 
         be_bc = const.tile([P, D], BF16, name="be_bc")
         gam_bc = const.tile([P, D], BF16, name="gam_bc")
 
-        def vecP():
-            spr["t"] = psum.tile([P, P], BF16, name="vt", tag="bank", bufs=6)
-            nc.tensor.transpose(spr["t"][:], vec[:], id_b[:])
+        def vecP(i):
+            spr["t", i] = rot(psum, [P, P], BF16, "bank", 6)
+            nc.tensor.transpose(spr["t", i][:], vec[i][:], id_b[:])
 
-        def vecS():
-            nc.scalar.copy(out=vcol[:], in_=spr["t"][:, 0:24])
+        def vecS(i):
+            nc.scalar.copy(out=vcol[:, 8 * i : 8 * (i + 1)], in_=spr["t", i][:, 0:8])
 
         def spread(i):
-            vb = (None, gam, bet)[i] if i else psum.tile([P, D], BF16, name="vb", tag="bank", bufs=6)
+            vb = (None, gam, bet)[i] if i else rot(psum, [P, D], BF16, "bank", 6)
             for m in range(8):
                 nc.tensor.transpose(vb[:, P * m : P * (m + 1)], vcol[:, 8 * i + m : 8 * i + m + 1].to_broadcast([P, P]), id_b[:])
             spr["v", i] = vb
@@ -221,7 +237,7 @@ def tile_linearattentionlayer_pb_kernel(tc, q_feat, kv, k_sum, audio, wo_bytes, 
 
         def wb_tile(r):
             if r not in wb:
-                wb[r] = work.tile([P, D], BF16, name="wb", bufs=4)
+                wb[r] = rot(work, [P, D], BF16, "wb", 4)
             return wb[r][:], wo8[r // 4][:, r % 4, :].bitcast(FP8)
 
         def castG(r):
@@ -237,7 +253,7 @@ def tile_linearattentionlayer_pb_kernel(tc, q_feat, kv, k_sum, audio, wo_bytes, 
             nc.scalar.copy(out=o, in_=i)
 
         def twP(rp, G):
-            xt = psum.tile([P, 2, 2, P], F32, name="tp", tag="bank", bufs=6)
+            xt = rot(psum, [P, 2, 2, P], F32, "bank", 6)
             xq[rp, G] = xt
             for k in range(2):
                 for u in range(2):
@@ -261,12 +277,12 @@ def tile_linearattentionlayer_pb_kernel(tc, q_feat, kv, k_sum, audio, wo_bytes, 
 
         def res(b, n):
             if (b, n) not in aa:
-                aa[b, n] = work.tile([P, D], F32, name="aa", bufs=4)
+                aa[b, n] = rot(work, [P, D], F32, "aa", 4)
             nc.gpsimd.tensor_tensor(out=aa[b, n][:], in0=au_raw[b, n][:], in1=bo_bc[:], op=ALU.add)
 
         def resV(b, n):
             if (b, n) not in aa:
-                aa[b, n] = work.tile([P, D], F32, name="aa", bufs=4)
+                aa[b, n] = rot(work, [P, D], F32, "aa", 4)
             nc.vector.tensor_tensor(out=aa[b, n][:], in0=au_raw[b, n][:], in1=bo_bc[:], op=ALU.add)
 
         y, x, xn, st, sv = {}, {}, {}, {}, {}
@@ -274,15 +290,15 @@ def tile_linearattentionlayer_pb_kernel(tc, q_feat, kv, k_sum, audio, wo_bytes, 
         def s2(b, n):
             o = P * (n % 2)
             for h in range(2):
-                y[b, n, h] = psum.tile([P, 512], F32, name="y", tag="bank", bufs=6)
+                y[b, n, h] = rot(psum, [P, 512], F32, "bank", 6)
                 for G in range(2):
                     ts = slice(256 * G + o, 256 * G + o + P)
                     ws = slice(512 * G, 512 * (G + 1))
                     nc.tensor.matmul_mx(out=y[b, n, h][:], lhsT=ac[b, n // 2][:, ts].bitcast(FP8X4), lhsT_scale=acs[b, n // 2][:, ts], rhs=wc[h][:, ws].bitcast(FP8X4), rhs_scale=wsc[h][:, ws], start=(G == 0), stop=(G == 1))
 
         def addx(b, n):
-            x[b, n] = work.tile([P, D], F32, name="x", bufs=3)
-            st[b, n] = work.tile([P, 8], F32, name="st", bufs=4)
+            x[b, n] = rot(work, [P, D], F32, "x", 3)
+            st[b, n] = rot(work, [P, 8], F32, "st", 4)
             for h in range(2):
                 hs = slice(512 * h, 512 * (h + 1))
                 nc.vector.scalar_tensor_tensor(out=x[b, n][:, hs], in0=y[b, n, h][:], scalar=1.0, in1=aa[b, n][:, hs], op0=ALU.mult, op1=ALU.add, accum_out=st[b, n][:, h : h + 1])
@@ -294,7 +310,7 @@ def tile_linearattentionlayer_pb_kernel(tc, q_feat, kv, k_sum, audio, wo_bytes, 
             nc.scalar.activation(out=st[b, n][:, 3:5], in_=st[b, n][:, 0:2], func=ACT.Copy, scale=-1.0 / D, accum_out=st[b, n][:, 2:3])
 
         def var(b, n):
-            sv[b, n] = work.tile([P, 8], F32, name="sv", bufs=4)
+            sv[b, n] = rot(work, [P, 8], F32, "sv", 4)
             junk = work.tile([P, D], BF16, name="junk", bufs=1)
             nc.scalar.activation(out=junk[:], in_=x[b, n][:], func=ACT.Square, bias=st[b, n][:, 2:3], accum_out=sv[b, n][:, 0:1])
 
@@ -303,7 +319,7 @@ def tile_linearattentionlayer_pb_kernel(tc, q_feat, kv, k_sum, audio, wo_bytes, 
 
         def cgam(b, n):
             if (b, n) not in xn:
-                xn[b, n] = work.tile([P, D], F32, name="xn", bufs=4)
+                xn[b, n] = rot(work, [P, D], F32, "xn", 4)
             nc.vector.scalar_tensor_tensor(out=xn[b, n][:], in0=x[b, n][:], scalar=st[b, n][:, 2:3], in1=gam[:], op0=ALU.add, op1=ALU.mult)
 
         def srs(b, n):
@@ -328,12 +344,12 @@ def tile_linearattentionlayer_pb_kernel(tc, q_feat, kv, k_sum, audio, wo_bytes, 
 
         def normS(b, n):
             if (b, n) not in xn:
-                xn[b, n] = work.tile([P, D], F32, name="xn", bufs=4)
+                xn[b, n] = rot(work, [P, D], F32, "xn", 4)
             nc.scalar.activation(out=xn[b, n][:], in_=x[b, n][:], func=ACT.Identity, scale=sv[b, n][:, 1:2], bias=sv[b, n][:, 2:3])
 
         def normV(b, n):
             if (b, n) not in xn:
-                xn[b, n] = work.tile([P, D], F32, name="xn", bufs=4)
+                xn[b, n] = rot(work, [P, D], F32, "xn", 4)
             nc.vector.tensor_scalar(out=xn[b, n][:], in0=x[b, n][:], scalar1=st[b, n][:, 2:3], scalar2=sv[b, n][:, 1:2], op0=ALU.add, op1=ALU.mult)
 
         def gG(b, n):
@@ -343,241 +359,244 @@ def tile_linearattentionlayer_pb_kernel(tc, q_feat, kv, k_sum, audio, wo_bytes, 
             nc.sync.dma_start(out=out[b, P * n : P * (n + 1), :], in_=xn[b, n][:])
 
         kvP(0, 0, 0, 1)
-        kvD(0, 0, 0, 0)
-        kvD(0, 0, 1, 0)
-        tqP(0, 0, 1)
         kvE(0, 0, 0, 1)
-        tqP(0, 0, 0)
+        tqP(0, 0, 1)
         tqS(0, 0, 1)
-        kvP(0, 0, 1, 1)
-        castV(0)
-        castV(1)
+        tqP(0, 0, 0)
+        tqS(0, 0, 0)
         tqP(0, 1, 1)
         tqP(0, 1, 0)
-        vecP()
-        tqS(0, 0, 0)
-        castS(3)
-        castS(2)
-        vecS()
-        tqS(0, 1, 0)
-        tqS(0, 1, 1)
-        kvE(0, 0, 1, 1)
-        twP(0, 1)
-        arsH(0, 1, 1, 1)
-        arsH(0, 1, 3, 0)
-        arsH(0, 0, 0, 1)
-        twP(0, 0)
-        arsH(0, 0, 1, 0)
-        kvD(0, 1, 0, 1)
-        kvP(0, 1, 0, 0)
-        qq(0, 0)
-        arsH(0, 0, 3, 1)
-        arsH(0, 1, 0, 1)
-        arsH(0, 0, 0, 0)
-        twP(1, 1)
-        arsH(0, 1, 2, 1)
-        twP(1, 0)
-        kvP(0, 1, 1, 1)
-        arsH(0, 0, 3, 0)
-        tqP(1, 0, 1)
-        kvD(0, 1, 1, 0)
-        spread(0)
-        arsH(0, 1, 2, 0)
-        kvP(1, 0, 0, 0)
-        twM(0, 0)
-        twM(0, 1)
-        arsH(0, 0, 2, 0)
-        tqS(1, 0, 1)
-        kvE(0, 1, 1, 1)
-        castG(6)
-        twM(1, 1)
-        castG(7)
-        kvE(0, 1, 0, 0)
-        tqP(1, 0, 0)
-        twM(1, 0)
-        wq(0)
-        tqS(1, 0, 0)
-        castG(4)
-        castG(5)
-        arsH(0, 0, 2, 1)
-        twP(3, 0)
-        arsH(0, 1, 0, 0)
-        arsH(0, 0, 1, 1)
-        kvP(1, 1, 1, 0)
-        kq(0, 1)
-        spreadS(0)
-        tqP(1, 1, 0)
-        tqS(1, 1, 0)
-        twP(2, 1)
-        qq(0, 1)
-        kvE(1, 1, 1, 0)
-        kvP(1, 1, 0, 1)
-        kvE(1, 0, 0, 0)
-        qq(1, 0)
-        arsH(0, 1, 3, 1)
         arsH(0, 1, 1, 0)
-        twP(3, 1)
-        kq(0, 0)
-        kvE(1, 1, 0, 1)
-        sq(0, 1)
-        twP(2, 0)
-        arsH(1, 1, 2, 0)
-        s1(0, 2, 1)
-        s1(0, 3, 1)
-        sq(0, 0)
-        arsH(1, 1, 0, 0)
-        s1(0, 3, 0)
-        s1(0, 2, 0)
-        res(0, 3)
-        arsH(1, 0, 0, 0)
-        twM(2, 1)
-        twM(3, 0)
-        s1(0, 0, 1)
-        twM(2, 0)
-        arsH(1, 0, 2, 0)
-        twM(3, 1)
-        mul(0, 2, 0)
-        mul(0, 2, 1)
-        mul(0, 3, 1)
-        s1(0, 1, 0)
-        arsH(1, 1, 3, 0)
-        arsH(1, 0, 0, 1)
-        s1(0, 1, 1)
-        arsH(1, 0, 3, 0)
-        s1(0, 0, 0)
-        kvP(1, 1, 0, 0)
-        mul(0, 3, 0)
-        mul(0, 0, 0)
-        kvP(1, 0, 1, 1)
+        kvP(0, 0, 1, 0)
+        arsH(0, 1, 0, 0)
+        kvD(0, 0, 0, 0)
+        arsH(0, 0, 2, 0)
+        kvD(0, 0, 1, 1)
+        castV(0)
+        arsH(0, 0, 0, 0)
+        arsH(0, 0, 3, 0)
+        arsH(0, 1, 3, 0)
+        castV(1)
+        arsH(0, 1, 2, 0)
+        kvE(0, 0, 1, 0)
+        castV(2)
+        twP(0, 1)
+        kvD(0, 1, 0, 0)
+        tqS(0, 1, 1)
+        twP(0, 0)
+        kvP(0, 1, 1, 1)
+        tqS(0, 1, 0)
+        castV(3)
+        kvD(0, 1, 0, 1)
+        twM(0, 0)
+        kvP(0, 1, 1, 0)
         tqP(1, 1, 1)
-        arsH(1, 0, 2, 1)
-        kvP(1, 0, 0, 1)
-        res(0, 2)
-        arsH(1, 0, 1, 0)
+        arsH(0, 0, 1, 0)
+        castS(7)
+        twP(1, 1)
+        kvE(0, 1, 1, 0)
+        kvE(0, 1, 1, 1)
+        tqP(1, 0, 1)
+        twM(0, 1)
+        twP(1, 0)
+        kvP(1, 0, 0, 0)
+        arsH(0, 1, 0, 1)
+        kq(0, 0)
+        vecP(0)
+        castS(6)
         tqS(1, 1, 1)
-        arsH(1, 1, 1, 0)
-        kvP(1, 0, 1, 0)
-        kvE(1, 1, 0, 0)
-        kvE(1, 0, 0, 1)
-        mul(0, 0, 1)
-        arsH(1, 0, 3, 1)
-        mul(0, 1, 1)
+        kvE(1, 0, 0, 0)
+        kvP(1, 1, 0, 1)
+        kq(0, 1)
         kvP(1, 1, 1, 1)
-        mul(0, 1, 0)
-        aq(0, 1)
-        aq(0, 0)
-        wq(1)
-        s2(0, 0)
-        kq(1, 0)
-        s2(0, 1)
-        qq(1, 1)
-        s1(1, 0, 0)
-        s2(0, 3)
-        kvE(1, 0, 1, 1)
-        arsH(1, 1, 1, 1)
+        twM(1, 0)
+        tqS(1, 0, 1)
+        vecS(0)
+        spread(0)
+        sq(0, 0)
+        twM(1, 1)
+        spreadS(0)
+        twP(3, 0)
+        qq(0, 0)
+        twP(3, 1)
+        s1(0, 0, 0)
+        wq(0)
+        kvE(1, 1, 0, 1)
         kvE(1, 1, 1, 1)
-        res(0, 1)
-        res(0, 0)
+        s1(0, 1, 0)
+        castS(5)
+        s1(0, 1, 1)
+        castS(4)
+        arsH(0, 0, 0, 1)
+        arsH(0, 0, 1, 1)
+        s1(0, 0, 1)
+        qq(0, 1)
+        arsH(0, 1, 1, 1)
+        arsH(0, 0, 2, 1)
+        arsH(0, 0, 3, 1)
+        twM(3, 0)
+        tqP(1, 0, 0)
+        twP(2, 0)
+        tqS(1, 0, 0)
+        twP(2, 1)
+        tqP(1, 1, 0)
+        kvP(1, 0, 1, 0)
+        twM(3, 1)
+        mul(0, 1, 0)
+        kvP(1, 0, 1, 1)
+        mul(0, 0, 0)
+        s1(0, 2, 1)
+        tqS(1, 1, 0)
+        arsH(0, 1, 2, 1)
+        arsH(0, 1, 3, 1)
+        mul(0, 0, 1)
+        mul(0, 1, 1)
+        twM(2, 1)
         kvE(1, 0, 1, 0)
-        arsH(1, 0, 1, 1)
-        addx(0, 0)
-        kq(1, 1)
-        s1(1, 1, 1)
-        addx(0, 3)
-        sq(1, 0)
-        s1(1, 1, 0)
-        nmuS(0, 0)
-        spread(1)
-        mul(1, 1, 1)
+        twM(2, 0)
+        s1(0, 3, 1)
+        qq(1, 1)
+        wq(1)
+        sq(0, 1)
+        arsH(1, 0, 3, 0)
+        res(0, 1)
+        s1(0, 2, 0)
+        arsH(1, 0, 2, 0)
+        kvE(1, 0, 1, 1)
+        qq(1, 0)
+        s1(0, 3, 0)
+        aq(0, 0)
+        res(0, 2)
+        kvP(1, 1, 1, 0)
+        res(0, 0)
         arsH(1, 1, 3, 1)
-        var(0, 0)
+        kvE(1, 1, 1, 0)
+        kvP(1, 0, 0, 1)
+        arsH(1, 0, 0, 1)
         res(1, 2)
-        nmuS(0, 3)
-        rstd(0, 0)
-        s2(0, 2)
-        mul(1, 0, 0)
-        s1(1, 0, 1)
-        spread(2)
-        s1(1, 2, 1)
-        spreadS(1)
-        addx(0, 1)
-        mul(1, 0, 1)
-        s1(1, 2, 0)
-        mul(1, 1, 0)
-        nmr(0, 0)
-        res(1, 0)
-        s1(1, 3, 0)
-        nmu(0, 1)
-        cgam(0, 1)
-        aq(1, 0)
-        normS(0, 0)
-        s2(1, 0)
+        mul(0, 3, 0)
+        mul(0, 2, 0)
+        kvP(1, 1, 0, 0)
+        arsH(1, 1, 1, 1)
+        mul(0, 2, 1)
+        vecP(1)
+        mul(0, 3, 1)
         arsH(1, 1, 0, 1)
-        var(0, 3)
+        arsH(1, 0, 1, 1)
+        vecP(2)
         arsH(1, 1, 2, 1)
-        rstd(0, 3)
-        s1(1, 3, 1)
+        s2(0, 1)
+        arsH(1, 0, 2, 1)
+        vecS(2)
+        kvE(1, 0, 0, 1)
+        kvE(1, 1, 0, 0)
+        kq(1, 1)
+        aq(0, 1)
+        s2(0, 2)
+        s2(0, 0)
+        arsH(1, 0, 1, 0)
+        vecS(1)
+        addx(0, 1)
+        kq(1, 0)
+        arsH(1, 0, 0, 0)
+        s1(1, 2, 1)
+        spread(2)
+        addx(0, 0)
+        arsH(1, 0, 3, 1)
+        arsH(1, 1, 2, 0)
+        s1(1, 2, 0)
         sq(1, 1)
-        spreadS(2)
         addx(0, 2)
-        mul(1, 2, 1)
-        nmuS(0, 2)
-        cgam(0, 3)
-        gG(0, 0)
-        var(0, 1)
-        rstd(0, 1)
-        s2(1, 1)
-        addx(1, 0)
+        nmuS(0, 0)
         mul(1, 2, 0)
-        var(0, 2)
+        s1(1, 3, 1)
+        arsH(1, 1, 1, 0)
+        s1(1, 3, 0)
+        var(0, 0)
+        nmuS(0, 1)
+        rstd(0, 0)
+        nmuS(0, 2)
+        s2(0, 3)
         res(1, 3)
-        nmuS(1, 0)
+        spread(1)
+        mul(1, 2, 1)
         mul(1, 3, 0)
         mul(1, 3, 1)
-        var(1, 0)
+        nmr(0, 0)
+        res(0, 3)
+        normS(0, 0)
+        spreadS(1)
+        var(0, 1)
         aq(1, 1)
-        srs(0, 1)
-        rstd(1, 0)
-        cgam(0, 2)
-        dbeta(0, 0)
-        nmr(1, 0)
         s2(1, 3)
-        dV(0, 3)
-        s2(1, 2)
+        cgam(0, 2)
+        cgam(0, 1)
+        arsH(1, 1, 0, 0)
+        s1(1, 1, 0)
+        gG(0, 0)
+        arsH(1, 1, 3, 0)
+        var(0, 2)
         rstd(0, 2)
-        normS(1, 0)
-        srs(0, 2)
+        addx(0, 3)
+        res(1, 0)
+        rstd(0, 1)
+        s2(1, 2)
+        spreadS(2)
+        s1(1, 0, 1)
+        s1(1, 1, 1)
+        s1(1, 0, 0)
         addx(1, 2)
-        nmuS(1, 2)
-        res(1, 1)
-        addx(1, 1)
-        var(1, 2)
+        sq(1, 0)
         addx(1, 3)
-        cgam(1, 2)
-        nmuS(1, 1)
-        var(1, 1)
-        store(0, 0)
+        mul(1, 0, 1)
+        nmuS(1, 2)
+        nmuS(0, 3)
+        mul(1, 1, 0)
+        var(0, 3)
+        dbeta(0, 0)
+        rstd(0, 3)
         nmuS(1, 3)
-        rstd(1, 1)
-        dbeta(0, 1)
-        rstd(1, 2)
-        srs(1, 2)
-        var(1, 3)
-        store(0, 1)
-        gG(1, 0)
-        cgam(1, 1)
-        store(0, 3)
-        dbeta(0, 2)
-        dbeta(1, 0)
-        rstd(1, 3)
+        mul(1, 0, 0)
+        mul(1, 1, 1)
+        store(0, 0)
+        res(1, 1)
+        nmr(0, 3)
+        normS(0, 3)
+        var(1, 2)
+        gG(0, 3)
+        aq(1, 0)
+        dV(0, 2)
+        dV(0, 1)
+        s2(1, 0)
+        s2(1, 1)
         store(0, 2)
-        dV(1, 1)
-        store(1, 0)
+        rstd(1, 2)
+        nmr(1, 2)
+        normS(1, 2)
+        addx(1, 1)
+        var(1, 3)
+        nmuS(1, 1)
+        addx(1, 0)
         cgam(1, 3)
-        dVh(1, 3, 0)
-        store(1, 1)
+        var(1, 1)
+        store(0, 1)
+        dbeta(0, 3)
+        nmuS(1, 0)
+        cgam(1, 1)
+        rstd(1, 3)
+        var(1, 0)
+        rstd(1, 1)
+        gG(1, 2)
         dbeta(1, 2)
-        store(1, 2)
-        storeh(1, 3, 0)
+        rstd(1, 0)
+        dVh(1, 3, 0)
         dVh(1, 3, 1)
+        store(0, 3)
+        storeh(1, 3, 0)
+        cgam(1, 0)
+        dV(1, 1)
         storeh(1, 3, 1)
+        store(1, 2)
+        store(1, 1)
+        dV(1, 0)
+        store(1, 0)

@@ -41,27 +41,31 @@ def tile_linearattentionlayer_pb_kernel(tc, q_feat, kv, k_sum, audio, wo_bytes, 
         q_raw, kv_raw, au_raw, wo8 = {}, {}, {}, {}
 
         def load_q(b, h):
-            t_ = rot(work, [P, 2, D], BF16, "q_raw", 3)
-            nc.sync.dma_start(out=t_[:], in_=q_feat[b, 256 * h : 256 * (h + 1), :].rearrange("(n p) k -> p n k", p=P))
+            t_ = rot(work, [P, 2, D], BF16, "q_raw", 2)
+            nc.sync.dma_start(out=t_[:], in_=q_feat[b, 256 * h : 256 * (h + 1), :].rearrange("(p n) k -> p n k", n=2))
             q_raw[b, h] = t_
 
-        def load_kv(b, g, c, parts=1):
-            src = kv[b].rearrange("(g p j) e -> g p j e", p=P, j=4)[g]
-            t_ = rot(work, [P, 4, 512], BF16, "kv_raw", 5)
-            w = 512 // parts
-            for i in range(parts):
-                nc.sync.dma_start(out=t_[:, :, w * i : w * (i + 1)], in_=src[:, :, 512 * c + w * i : 512 * c + w * (i + 1)])
-            kv_raw[b, g, c] = t_
+        def load_kv(b, g):
+            t_ = rot(work, [P, 4, D], BF16, "kv_raw", 2)
+            nc.sync.dma_start(out=t_[:], in_=kv[b].rearrange("(g p j) e -> g p j e", p=P, j=4)[g])
+            for c in range(2):
+                kv_raw[b, g, c] = t_[:, :, 512 * c : 512 * (c + 1)]
+
+        def load_kv0(c):
+            t_ = const.tile([P, 4, 512], BF16, name="kv0_%d" % c)
+            nc.sync.dma_start(out=t_[:], in_=kv[0].rearrange("(g p j) e -> g p j e", p=P, j=4)[0][:, :, 512 * c : 512 * (c + 1)])
+            kv_raw[0, 0, c] = t_[:]
 
         def load_wo(h):
             t_ = const.tile([P, 4, D], U8, name="wo8_%d" % h)
             nc.sync.dma_start(out=t_[:], in_=wo_bytes[512 * h : 512 * (h + 1), :].rearrange("(r p) e -> p r e", p=P))
             wo8[h] = t_
 
-        def load_audio(b, n):
-            t_ = rot(work, [P, D], BF16, "au", 6)
-            nc.sync.dma_start(out=t_[:], in_=audio[b, P * n : P * (n + 1), :])
-            au_raw[b, n] = t_
+        def load_audio(b, h):
+            t_ = rot(work, [P, 2, D], BF16, "au", 3)
+            nc.sync.dma_start(out=t_[:], in_=audio[b, 256 * h : 256 * (h + 1), :].rearrange("(p n) k -> p n k", n=2))
+            for i in range(2):
+                au_raw[b, 2 * h + i] = t_[:, i, :]
 
         scol = const.tile([P, 8], F32, name="scol")
         vec = {}
@@ -74,30 +78,30 @@ def tile_linearattentionlayer_pb_kernel(tc, q_feat, kv, k_sum, audio, wo_bytes, 
         ks_b = const.tile([P, 16], BF16, name="ks_b")
         make_identity(nc, id_f[:])
         make_identity(nc, id_b[:])
-        load_kv(0, 0, 0)
+        nc.sync.dma_start(out=scol[:], in_=wo_scale.rearrange("o (m p) -> p (o m)", p=P))
+        load_kv0(0)
         load_q(0, 0)
         nc.sync.dma_start(out=ks_b[:].rearrange("p (b g t) -> p b g t", b=2, g=2), in_=k_sum.rearrange("b (g p t) -> p b g t", p=P, t=4))
-        nc.sync.dma_start(out=scol[:].rearrange("p (g t) -> p g t", g=2), in_=wo_scale.rearrange("o (g p t) -> p (o g) t", p=P, t=4))
-        load_kv(0, 0, 1)
+        load_kv0(1)
         load_q(0, 1)
+        load_kv(0, 1)
         load_wo(0)
-        load_kv(0, 1, 0)
-        load_kv(0, 1, 1)
         load_wo(1)
         load_q(1, 0)
         load_q(1, 1)
-        for g, c in ((0, 0), (1, 0), (0, 1), (1, 1)):
-            load_kv(1, g, c)
+        load_kv(1, 0)
+        load_kv(1, 1)
+
         def load_vec(i, v):
             nc.sync.dma_start(out=vec[i][0:8, :], in_=v.rearrange("(m n) -> m n", n=P))
 
         load_vec(0, bo)
-        for n in range(4):
-            load_audio(0, n)
+        for h in range(2):
+            load_audio(0, h)
         load_vec(1, gamma)
         load_vec(2, beta)
-        for n in range(4):
-            load_audio(1, n)
+        for h in range(2):
+            load_audio(1, h)
         ks_f = const.tile([P, 16], F32, name="ks_f")
         eps = const.tile([P, 2], F32, name="eps")
         nc.gpsimd.tensor_scalar(out=eps[:, 0:1], in0=id_f[:, 0:1], scalar1=0.0, scalar2=1e-6, op0=ALU.mult, op1=ALU.add)
@@ -138,29 +142,25 @@ def tile_linearattentionlayer_pb_kernel(tc, q_feat, kv, k_sum, audio, wo_bytes, 
                 grp[b, c] = rot(work, [P, 4096], BF16, "kvg", 2, align_bytes=64)
             return grp[b, c][:, 2048 * g : 2048 * (g + 1)]
 
+        def kvV(b, g, c, k):
+            dst = kv_dst(b, g, c).rearrange("p (t m j) -> p t m j", t=4, j=4)
+            nc.vector.tensor_copy(out=dst, in_=kv_raw[b, g, c].rearrange("p j (m t) -> p t m j", t=4))
+
         def kvD(b, g, c, k):
             dst = kv_dst(b, g, c).rearrange("p (t m j) -> p t m j", t=4, j=4)
-            src = kv_raw[b, g, c][:].rearrange("p j (m t) -> p t m j", t=4)
+            src = kv_raw[b, g, c].rearrange("p j (m t) -> p t m j", t=4)
             nc.vector.tensor_copy(out=dst[:, 2 * k : 2 * k + 2], in_=src[:, 2 * k : 2 * k + 2])
-
-        def kvS(b, g, c, k):
-            dst = kv_dst(b, g, c).rearrange("p (t m j) -> p t m j", t=4, j=4)
-            src = kv_raw[b, g, c][:].rearrange("p j (m t) -> p t m j", t=4)
-            nc.scalar.copy(out=dst[:, 2 * k : 2 * k + 2], in_=src[:, 2 * k : 2 * k + 2])
 
         def kvP(b, g, c, k):
             if (b, g, c, k) not in ibs:
                 ibs[b, g, c, k] = rot(psum, [P, D], BF16, "bank", 6)
             ib = ibs[b, g, c, k]
-            src = kv_raw[b, g, c][:].rearrange("p j (m t) -> p t m j", t=4)
+            src = kv_raw[b, g, c].rearrange("p j (m t) -> p t m j", t=4)
             for t in range(2):
                 nc.tensor.matmul(ib[:, 512 * t : 512 * (t + 1)], id_b[:], src[:, 2 * k + t], start=True, stop=True)
 
         def kvE(b, g, c, k):
             nc.scalar.copy(out=kv_dst(b, g, c)[:, 1024 * k : 1024 * (k + 1)], in_=ibs[b, g, c, k][:])
-
-        def kvF(b, g, c, k):
-            nc.vector.tensor_copy(out=kv_dst(b, g, c)[:, 1024 * k : 1024 * (k + 1)], in_=ibs[b, g, c, k][:])
 
         def kq(b, c):
             kc[b, c] = rot(work, [P, D], U32, "kc", 4, align_bytes=64)
@@ -179,10 +179,6 @@ def tile_linearattentionlayer_pb_kernel(tc, q_feat, kv, k_sum, audio, wo_bytes, 
         def sq(b, h):
             r = rr[b, h][:]
             nc.scalar.activation(out=r, in_=r, func=ACT.Square)
-
-        def sqV(b, h):
-            r = rr[b, h][:]
-            nc.vector.tensor_tensor(out=r, in0=r, in1=r, op=ALU.mult)
 
         at, ac, acs, num = {}, {}, {}, {}
 
@@ -209,10 +205,19 @@ def tile_linearattentionlayer_pb_kernel(tc, q_feat, kv, k_sum, audio, wo_bytes, 
         gam = psum.tile([P, D], BF16, name="gam", bufs=1)
         bet = psum.tile([P, D], BF16, name="bet", bufs=1)
         spr = {}
+        sc_bc = const.tile([P, D], F32, name="sc_bc")
+
+        def spsP(h):
+            spr[h] = rot(psum, [P, 512], F32, "bank", 6)
+            for m in range(4):
+                nc.tensor.transpose(spr[h][:, P * m : P * (m + 1)], scol[:, 4 * h + m : 4 * h + m + 1].to_broadcast([P, P]), id_f[:])
+
+        def spsS(h):
+            nc.scalar.copy(out=sc_bc[:, 512 * h : 512 * (h + 1)], in_=spr[h][:])
+
 
         bo_bc = const.tile([P, D], BF16, name="bo_bc")
         be_bc = const.tile([P, D], BF16, name="be_bc")
-        gam_bc = const.tile([P, D], BF16, name="gam_bc")
 
         def vecP(i):
             spr["t", i] = rot(psum, [P, P], BF16, "bank", 6)
@@ -227,63 +232,57 @@ def tile_linearattentionlayer_pb_kernel(tc, q_feat, kv, k_sum, audio, wo_bytes, 
                 nc.tensor.transpose(vb[:, P * m : P * (m + 1)], vcol[:, 8 * i + m : 8 * i + m + 1].to_broadcast([P, P]), id_b[:])
             spr["v", i] = vb
 
-        def spreadV(i):
-            nc.vector.tensor_copy(out=(bo_bc, gam_bc, be_bc)[i][:], in_=spr["v", i][:])
-
         def spreadS(i):
-            nc.scalar.copy(out=(bo_bc, gam_bc, be_bc)[i][:], in_=spr["v", i][:])
+            nc.scalar.copy(out=(bo_bc, None, be_bc)[i][:], in_=spr["v", i][:])
 
         wc, wsc, gw, wb = {}, {}, {}, {}
 
-        def wb_tile(r):
-            if r not in wb:
-                wb[r] = rot(work, [P, D], BF16, "wb", 4)
-            return wb[r][:], wo8[r // 4][:, r % 4, :].bitcast(FP8)
-
-        def castG(r):
-            o, i = wb_tile(r)
-            nc.gpsimd.tensor_copy(out=o, in_=i)
-
-        def castV(r):
-            o, i = wb_tile(r)
-            nc.vector.tensor_copy(out=o, in_=i)
-
-        def castS(r):
-            o, i = wb_tile(r)
-            nc.scalar.copy(out=o, in_=i)
+        def wo(r):
+            wb[r] = rot(work, [P, D], BF16, "wb", 4)
+            nc.vector.tensor_tensor(out=wb[r][:], in0=wo8[r // 4][:, r % 4, :].bitcast(FP8), in1=sc_bc[:], op=ALU.mult)
 
         def twP(rp, G):
             xt = rot(psum, [P, 2, 2, P], F32, "bank", 6)
             xq[rp, G] = xt
             for k in range(2):
                 for u in range(2):
-                    nc.tensor.transpose(xt[:, u, k, :], words(wb[2 * rp + k][:])[:, 256 * G + u : 256 * (G + 1) : 2], id_f[:])
+                    nc.tensor.transpose(xt[:, k, u, :], words(wb[2 * rp + k][:])[:, 256 * G + u : 256 * (G + 1) : 2], id_f[:])
 
-        def twM(rp, G):
+        def tw_dst(rp, G):
             h, i = rp // 2, rp % 2
             if h not in gw:
                 gw[h] = work.tile([P, 4096], BF16, name="gw", bufs=1, align_bytes=64)
             o = 2048 * G + 1024 * i
-            sc = scol[:, 4 * G : 4 * G + 4].rearrange("p (u v) -> p u v", u=2).unsqueeze(1).to_broadcast([P, 2 * P, 2, 2])
-            src = xq[rp, G][:].rearrange("p u k r -> p (u k r)").bitcast(BF16).rearrange("p (u f v) -> p f u v", u=2, v=2)
-            nc.vector.tensor_tensor(out=gw[h][:, o : o + 1024].rearrange("p (f u v) -> p f u v", u=2, v=2), in0=src, in1=sc, op=ALU.mult)
+            return words(gw[h][:, o : o + 1024]).rearrange("p (n r u) -> p n r u", n=2, u=2), xq[rp, G][:].rearrange("p n u r -> p n r u")
+
+        def twS(rp, G):
+            o, i = tw_dst(rp, G)
+            nc.scalar.copy(out=o, in_=i)
 
         def wq(h):
             wc[h] = const.tile([P, D], U32, name="wc%d" % h, align_bytes=64)
             wsc[h] = const.tile([P, D], U8, name="wsc%d" % h, align_bytes=64)
             nc.vector.quantize_mx(out=wc[h][:].bitcast(FP8X4), scales=wsc[h][:], in_=gw[h][:])
 
-        aa = {}
+        aa, z = {}, {}
 
         def res(b, n):
             if (b, n) not in aa:
                 aa[b, n] = rot(work, [P, D], F32, "aa", 4)
-            nc.gpsimd.tensor_tensor(out=aa[b, n][:], in0=au_raw[b, n][:], in1=bo_bc[:], op=ALU.add)
+            nc.gpsimd.tensor_tensor(out=aa[b, n][:], in0=au_raw[b, n], in1=bo_bc[:], op=ALU.add)
 
-        def resV(b, n):
+        def zP(b, n):
+            for h in range(2):
+                hs = slice(512 * h, 512 * (h + 1))
+                z[b, n, h] = rot(psum, [P, 512], F32, "bank", 6)
+                nc.tensor.matmul(z[b, n, h][:], id_b[:], au_raw[b, n][:, hs], start=True, stop=False)
+                nc.tensor.matmul(z[b, n, h][:], id_b[:], bo_bc[:, hs], start=False, stop=True)
+
+        def zS(b, n):
             if (b, n) not in aa:
                 aa[b, n] = rot(work, [P, D], F32, "aa", 4)
-            nc.vector.tensor_tensor(out=aa[b, n][:], in0=au_raw[b, n][:], in1=bo_bc[:], op=ALU.add)
+            for h in range(2):
+                nc.scalar.copy(out=aa[b, n][:, 512 * h : 512 * (h + 1)], in_=z[b, n, h][:])
 
         y, x, xn, st, sv = {}, {}, {}, {}, {}
 
@@ -335,268 +334,248 @@ def tile_linearattentionlayer_pb_kernel(tc, q_feat, kv, k_sum, audio, wo_bytes, 
             hs = slice(512 * h, 512 * (h + 1))
             nc.vector.scalar_tensor_tensor(out=xn[b, n][:, hs], in0=xn[b, n][:, hs], scalar=sv[b, n][:, 1:2], in1=bet[:, hs], op0=ALU.mult, op1=ALU.add)
 
+        def rows(b, n):
+            h, i = n // 2, n % 2
+            return out[b, 256 * h : 256 * (h + 1), :].rearrange("(p n) k -> n p k", n=2)[i]
+
         def storeh(b, n, h):
             hs = slice(512 * h, 512 * (h + 1))
-            nc.sync.dma_start(out=out[b, P * n : P * (n + 1), hs], in_=xn[b, n][:, hs])
-
-        def nmr(b, n):
-            nc.scalar.activation(out=sv[b, n][:, 2:3], in_=st[b, n][:, 2:3], func=ACT.Copy, scale=sv[b, n][:, 1:2])
-
-        def normS(b, n):
-            if (b, n) not in xn:
-                xn[b, n] = rot(work, [P, D], F32, "xn", 4)
-            nc.scalar.activation(out=xn[b, n][:], in_=x[b, n][:], func=ACT.Identity, scale=sv[b, n][:, 1:2], bias=sv[b, n][:, 2:3])
-
-        def normV(b, n):
-            if (b, n) not in xn:
-                xn[b, n] = rot(work, [P, D], F32, "xn", 4)
-            nc.vector.tensor_scalar(out=xn[b, n][:], in0=x[b, n][:], scalar1=st[b, n][:, 2:3], scalar2=sv[b, n][:, 1:2], op0=ALU.add, op1=ALU.mult)
-
-        def gG(b, n):
-            nc.gpsimd.tensor_tensor(out=xn[b, n][:], in0=xn[b, n][:], in1=gam_bc[:], op=ALU.mult)
+            nc.sync.dma_start(out=rows(b, n)[:, hs], in_=xn[b, n][:, hs])
 
         def store(b, n):
-            nc.sync.dma_start(out=out[b, P * n : P * (n + 1), :], in_=xn[b, n][:])
+            nc.sync.dma_start(out=rows(b, n), in_=xn[b, n][:])
 
-        kvP(0, 0, 0, 1)
-        kvE(0, 0, 0, 1)
-        tqP(0, 0, 1)
-        tqS(0, 0, 1)
+        spsP(1)
+        spsP(0)
         tqP(0, 0, 0)
-        tqS(0, 0, 0)
+        spsS(1)
+        tqP(0, 0, 1)
+        spsS(0)
         tqP(0, 1, 1)
-        tqP(0, 1, 0)
-        arsH(0, 1, 1, 0)
-        kvP(0, 0, 1, 0)
-        arsH(0, 1, 0, 0)
-        kvD(0, 0, 0, 0)
+        kvV(0, 0, 0, 0)
+        tqS(0, 0, 0)
         arsH(0, 0, 2, 0)
-        kvD(0, 0, 1, 1)
-        castV(0)
-        arsH(0, 0, 0, 0)
+        kvV(0, 0, 1, 0)
+        tqP(0, 1, 0)
+        tqS(0, 0, 1)
         arsH(0, 0, 3, 0)
-        arsH(0, 1, 3, 0)
-        castV(1)
-        arsH(0, 1, 2, 0)
-        kvE(0, 0, 1, 0)
-        castV(2)
-        twP(0, 1)
-        kvD(0, 1, 0, 0)
-        tqS(0, 1, 1)
-        twP(0, 0)
-        kvP(0, 1, 1, 1)
-        tqS(0, 1, 0)
-        castV(3)
-        kvD(0, 1, 0, 1)
-        twM(0, 0)
         kvP(0, 1, 1, 0)
-        tqP(1, 1, 1)
-        arsH(0, 0, 1, 0)
-        castS(7)
-        twP(1, 1)
-        kvE(0, 1, 1, 0)
-        kvE(0, 1, 1, 1)
-        tqP(1, 0, 1)
-        twM(0, 1)
-        twP(1, 0)
-        kvP(1, 0, 0, 0)
-        arsH(0, 1, 0, 1)
-        kq(0, 0)
-        vecP(0)
-        castS(6)
-        tqS(1, 1, 1)
-        kvE(1, 0, 0, 0)
-        kvP(1, 1, 0, 1)
-        kq(0, 1)
-        kvP(1, 1, 1, 1)
-        twM(1, 0)
-        tqS(1, 0, 1)
-        vecS(0)
-        spread(0)
-        sq(0, 0)
-        twM(1, 1)
-        spreadS(0)
-        twP(3, 0)
+        arsH(0, 1, 1, 0)
+        arsH(0, 1, 2, 0)
         qq(0, 0)
-        twP(3, 1)
-        s1(0, 0, 0)
-        wq(0)
-        kvE(1, 1, 0, 1)
-        kvE(1, 1, 1, 1)
-        s1(0, 1, 0)
-        castS(5)
-        s1(0, 1, 1)
-        castS(4)
-        arsH(0, 0, 0, 1)
-        arsH(0, 0, 1, 1)
-        s1(0, 0, 1)
+        arsH(0, 1, 0, 0)
+        kvP(0, 1, 1, 1)
+        tqV(0, 1, 1)
+        kvV(0, 1, 0, 0)
+        arsH(0, 1, 0, 1)
+        arsH(0, 1, 3, 0)
+        tqS(0, 1, 0)
         qq(0, 1)
+        arsH(0, 0, 1, 0)
+        wo(0)
+        wo(1)
+        wo(3)
+        arsH(0, 0, 0, 0)
+        twP(0, 0)
         arsH(0, 1, 1, 1)
         arsH(0, 0, 2, 1)
-        arsH(0, 0, 3, 1)
-        twM(3, 0)
-        tqP(1, 0, 0)
-        twP(2, 0)
-        tqS(1, 0, 0)
-        twP(2, 1)
-        tqP(1, 1, 0)
-        kvP(1, 0, 1, 0)
-        twM(3, 1)
-        mul(0, 1, 0)
-        kvP(1, 0, 1, 1)
-        mul(0, 0, 0)
-        s1(0, 2, 1)
-        tqS(1, 1, 0)
-        arsH(0, 1, 2, 1)
         arsH(0, 1, 3, 1)
-        mul(0, 0, 1)
-        mul(0, 1, 1)
-        twM(2, 1)
-        kvE(1, 0, 1, 0)
-        twM(2, 0)
-        s1(0, 3, 1)
-        qq(1, 1)
-        wq(1)
-        sq(0, 1)
-        arsH(1, 0, 3, 0)
-        res(0, 1)
-        s1(0, 2, 0)
-        arsH(1, 0, 2, 0)
-        kvE(1, 0, 1, 1)
-        qq(1, 0)
-        s1(0, 3, 0)
-        aq(0, 0)
-        res(0, 2)
-        kvP(1, 1, 1, 0)
-        res(0, 0)
-        arsH(1, 1, 3, 1)
-        kvE(1, 1, 1, 0)
-        kvP(1, 0, 0, 1)
-        arsH(1, 0, 0, 1)
-        res(1, 2)
-        mul(0, 3, 0)
-        mul(0, 2, 0)
-        kvP(1, 1, 0, 0)
-        arsH(1, 1, 1, 1)
-        mul(0, 2, 1)
-        vecP(1)
-        mul(0, 3, 1)
-        arsH(1, 1, 0, 1)
+        arsH(0, 0, 1, 1)
+        sq(0, 0)
+        twP(0, 1)
+        wo(2)
+        tqP(1, 1, 1)
+        kq(0, 0)
+        kvE(0, 1, 1, 0)
+        kvE(0, 1, 1, 1)
+        wo(5)
+        tqP(1, 1, 0)
+        twS(0, 0)
+        twP(1, 1)
+        kvD(1, 0, 1, 0)
+        twP(1, 0)
+        arsH(0, 0, 0, 1)
+        wo(6)
+        tqS(1, 1, 1)
+        tqS(1, 1, 0)
+        twS(0, 1)
+        kq(0, 1)
+        tqP(1, 0, 0)
+        wo(7)
         arsH(1, 0, 1, 1)
-        vecP(2)
+        vecP(0)
+        twS(1, 0)
+        tqP(1, 0, 1)
+        twS(1, 1)
+        vecS(0)
+        arsH(1, 1, 1, 1)
+        s1(0, 1, 1)
+        arsH(1, 0, 0, 1)
+        tqS(1, 0, 1)
         arsH(1, 1, 2, 1)
-        s2(0, 1)
-        arsH(1, 0, 2, 1)
-        vecS(2)
-        kvE(1, 0, 0, 1)
-        kvE(1, 1, 0, 0)
-        kq(1, 1)
-        aq(0, 1)
-        s2(0, 2)
-        s2(0, 0)
-        arsH(1, 0, 1, 0)
-        vecS(1)
-        addx(0, 1)
-        kq(1, 0)
-        arsH(1, 0, 0, 0)
-        s1(1, 2, 1)
-        spread(2)
-        addx(0, 0)
+        s1(0, 1, 0)
         arsH(1, 0, 3, 1)
-        arsH(1, 1, 2, 0)
-        s1(1, 2, 0)
-        sq(1, 1)
-        addx(0, 2)
-        nmuS(0, 0)
-        mul(1, 2, 0)
-        s1(1, 3, 1)
+        tqS(1, 0, 0)
+        spread(0)
+        wq(0)
+        s1(0, 0, 1)
+        arsH(0, 0, 3, 1)
+        arsH(1, 1, 0, 1)
+        arsH(0, 1, 2, 1)
+        s1(0, 0, 0)
+        s1(0, 2, 0)
+        kvD(1, 0, 0, 0)
+        s1(0, 3, 0)
+        wo(4)
+        kvV(1, 1, 0, 0)
+        twP(2, 1)
+        arsH(1, 1, 3, 1)
+        spreadS(0)
+        sq(0, 1)
+        arsH(1, 0, 2, 1)
+        mul(0, 1, 1)
+        mul(0, 1, 0)
+        twP(3, 0)
+        twS(2, 1)
+        s1(0, 3, 1)
+        s1(0, 2, 1)
+        vecP(1)
         arsH(1, 1, 1, 0)
-        s1(1, 3, 0)
-        var(0, 0)
-        nmuS(0, 1)
-        rstd(0, 0)
-        nmuS(0, 2)
-        s2(0, 3)
-        res(1, 3)
-        spread(1)
-        mul(1, 2, 1)
-        mul(1, 3, 0)
-        mul(1, 3, 1)
-        nmr(0, 0)
-        res(0, 3)
-        normS(0, 0)
-        spreadS(1)
-        var(0, 1)
-        aq(1, 1)
-        s2(1, 3)
-        cgam(0, 2)
-        cgam(0, 1)
+        mul(0, 0, 1)
+        mul(0, 0, 0)
+        mul(0, 2, 0)
+        arsH(1, 0, 0, 0)
+        twS(3, 0)
+        mul(0, 3, 0)
+        vecS(1)
+        arsH(1, 0, 2, 0)
+        arsH(1, 0, 1, 0)
         arsH(1, 1, 0, 0)
-        s1(1, 1, 0)
-        gG(0, 0)
+        mul(0, 3, 1)
         arsH(1, 1, 3, 0)
-        var(0, 2)
-        rstd(0, 2)
+        arsH(1, 1, 2, 0)
+        mul(0, 2, 1)
+        aq(0, 0)
+        kvP(1, 0, 1, 1)
+        twP(3, 1)
+        kvE(1, 0, 1, 1)
+        twP(2, 0)
+        twS(2, 0)
+        qq(1, 1)
+        kvP(1, 0, 0, 1)
+        twS(3, 1)
+        kvV(1, 1, 1, 0)
+        aq(0, 1)
+        res(0, 3)
+        vecP(2)
+        kvE(1, 0, 0, 1)
+        vecS(2)
+        zP(0, 2)
+        kq(1, 1)
+        wq(1)
+        zS(0, 2)
+        zP(0, 1)
+        s2(0, 3)
+        kq(1, 0)
+        zS(0, 1)
         addx(0, 3)
+        s2(0, 2)
+        sq(1, 1)
+        s1(1, 2, 0)
+        s2(0, 1)
+        nmuS(0, 3)
+        arsH(1, 0, 3, 0)
+        s1(1, 3, 1)
+        s1(1, 3, 0)
+        qq(1, 0)
+        spread(1)
+        addx(0, 2)
+        addx(0, 1)
+        mul(1, 3, 1)
+        mul(1, 2, 0)
+        nmuS(0, 2)
+        var(0, 3)
+        s1(1, 2, 1)
+        nmuS(0, 1)
+        cgam(0, 3)
+        rstd(0, 3)
+        var(0, 1)
+        s2(0, 0)
+        sq(1, 0)
+        s1(1, 1, 1)
+        var(0, 2)
+        s1(1, 0, 1)
+        srs(0, 3)
+        mul(1, 3, 0)
+        mul(1, 2, 1)
+        res(0, 0)
+        res(1, 3)
+        res(1, 2)
+        addx(0, 0)
+        aq(1, 1)
+        mul(1, 0, 1)
+        s1(1, 1, 0)
+        nmuS(0, 0)
+        rstd(0, 2)
+        spread(2)
+        mul(1, 1, 0)
+        s1(1, 0, 0)
+        mul(1, 0, 0)
+        s2(1, 3)
         res(1, 0)
+        mul(1, 1, 1)
+        res(1, 1)
+        cgam(0, 2)
+        cgam(0, 0)
+        aq(1, 0)
+        spreadS(2)
+        var(0, 0)
+        rstd(0, 0)
+        cgam(0, 1)
         rstd(0, 1)
         s2(1, 2)
-        spreadS(2)
-        s1(1, 0, 1)
-        s1(1, 1, 1)
-        s1(1, 0, 0)
-        addx(1, 2)
-        sq(1, 0)
-        addx(1, 3)
-        mul(1, 0, 1)
-        nmuS(1, 2)
-        nmuS(0, 3)
-        mul(1, 1, 0)
-        var(0, 3)
-        dbeta(0, 0)
-        rstd(0, 3)
-        nmuS(1, 3)
-        mul(1, 0, 0)
-        mul(1, 1, 1)
-        store(0, 0)
-        res(1, 1)
-        nmr(0, 3)
-        normS(0, 3)
-        var(1, 2)
-        gG(0, 3)
-        aq(1, 0)
-        dV(0, 2)
-        dV(0, 1)
         s2(1, 0)
-        s2(1, 1)
-        store(0, 2)
-        rstd(1, 2)
-        nmr(1, 2)
-        normS(1, 2)
-        addx(1, 1)
-        var(1, 3)
-        nmuS(1, 1)
+        srs(0, 2)
         addx(1, 0)
-        cgam(1, 3)
-        var(1, 1)
-        store(0, 1)
-        dbeta(0, 3)
+        addx(1, 2)
+        srs(0, 0)
+        srs(0, 1)
         nmuS(1, 0)
-        cgam(1, 1)
-        rstd(1, 3)
+        dbeta(0, 3)
+        addx(1, 3)
         var(1, 0)
-        rstd(1, 1)
-        gG(1, 2)
-        dbeta(1, 2)
+        dbeta(0, 2)
+        nmuS(1, 2)
+        s2(1, 1)
+        var(1, 2)
+        cgam(1, 0)
+        cgam(1, 2)
         rstd(1, 0)
+        addx(1, 1)
+        nmuS(1, 3)
+        rstd(1, 2)
+        srs(1, 0)
+        cgam(1, 3)
+        dbeta(0, 0)
+        dbeta(0, 1)
+        nmu(1, 1)
+        var(1, 3)
+        srs(1, 2)
+        rstd(1, 3)
+        store(0, 3)
+        store(0, 2)
+        dbeta(1, 0)
+        store(0, 0)
         dVh(1, 3, 0)
         dVh(1, 3, 1)
-        store(0, 3)
+        var(1, 1)
+        store(0, 1)
+        store(1, 0)
+        rstd(1, 1)
         storeh(1, 3, 0)
-        cgam(1, 0)
-        dV(1, 1)
         storeh(1, 3, 1)
+        cgam(1, 1)
+        dbeta(1, 2)
+        dV(1, 1)
         store(1, 2)
         store(1, 1)
-        dV(1, 0)
-        store(1, 0)

from contextlib import ExitStack

import concourse.mybir as mybir
from concourse.masks import make_identity

B, T, D = 2, 512, 1024
P = 128
FLOPS = 2 * 2 * B * T * D * D

F32 = mybir.dt.float32
BF16 = mybir.dt.bfloat16
U32 = mybir.dt.uint32
U8 = mybir.dt.uint8
FP8 = mybir.dt.float8_e4m3fn
FP8X4 = mybir.dt.float8_e4m3fn_x4
ALU = mybir.AluOpType
ACT = mybir.ActivationFunctionType


def words(ap):
    return ap.bitcast(F32)


def tile_linearattentionlayer_pb_kernel(tc, q_feat, kv, k_sum, audio, wo_bytes, wo_scale, bo, gamma, beta, out):
    nc = tc.nc
    with ExitStack() as ctx:
        const = ctx.enter_context(tc.tile_pool(name="const", bufs=1))
        work = ctx.enter_context(tc.tile_pool(name="work", bufs=2))
        psum = ctx.enter_context(tc.psum_pool(name="psum", bufs=1))
        ctx.enter_context(tc.manual_schedule())

        count = {}

        def rot(pool, shape, dtype, name, n, align_bytes=None):
            i = count.setdefault(name, 0)
            count[name] = i + 1
            if align_bytes is None:
                return pool.tile(shape, dtype, name=name, tag="%s_%d_%d" % (name, i % n, n), bufs=1)
            return pool.tile(shape, dtype, name=name, tag="%s_%d_%d" % (name, i % n, n), bufs=1, align_bytes=align_bytes)

        q_raw, kv_raw, au_raw, wo8 = {}, {}, {}, {}

        def load_q(b, h):
            t_ = rot(work, [P, 2, D], BF16, "q_raw", 2)
            nc.sync.dma_start(out=t_[:], in_=q_feat[b, 256 * h : 256 * (h + 1), :].rearrange("(p n) k -> p n k", n=2))
            q_raw[b, h] = t_

        def load_kv(b, g):
            t_ = rot(work, [P, 4, D], BF16, "kv_raw", 2)
            nc.sync.dma_start(out=t_[:], in_=kv[b].rearrange("(g p j) e -> g p j e", p=P, j=4)[g])
            for c in range(2):
                kv_raw[b, g, c] = t_[:, :, 512 * c : 512 * (c + 1)]

        def load_kv0(c):
            t_ = const.tile([P, 4, 512], BF16, name="kv0_%d" % c)
            nc.sync.dma_start(out=t_[:], in_=kv[0].rearrange("(g p j) e -> g p j e", p=P, j=4)[0][:, :, 512 * c : 512 * (c + 1)])
            kv_raw[0, 0, c] = t_[:]

        def load_wo(h):
            t_ = const.tile([P, 4, D], U8, name="wo8_%d" % h)
            nc.sync.dma_start(out=t_[:], in_=wo_bytes[512 * h : 512 * (h + 1), :].rearrange("(r p) e -> p r e", p=P))
            wo8[h] = t_

        def load_audio(b, h):
            t_ = rot(work, [P, 2, D], BF16, "au", 3)
            nc.sync.dma_start(out=t_[:], in_=audio[b, 256 * h : 256 * (h + 1), :].rearrange("(p n) k -> p n k", n=2))
            for i in range(2):
                au_raw[b, 2 * h + i] = t_[:, i, :]

        scol = const.tile([P, 8], F32, name="scol")
        vec = {}
        for i in range(3):
            vec[i] = const.tile([P, P], BF16, name="vec%d" % i)
            nc.vector.memset(vec[i][:], 0.0)
        vcol = const.tile([P, 24], BF16, name="vcol")
        id_f = const.tile([P, P], F32, name="id_f")
        id_b = const.tile([P, P], BF16, name="id_b")
        ks_b = const.tile([P, 16], BF16, name="ks_b")
        make_identity(nc, id_f[:])
        make_identity(nc, id_b[:])
        nc.sync.dma_start(out=scol[:], in_=wo_scale.rearrange("o (m p) -> p (o m)", p=P))
        load_kv0(0)
        load_q(0, 0)
        nc.sync.dma_start(out=ks_b[:].rearrange("p (b g t) -> p b g t", b=2, g=2), in_=k_sum.rearrange("b (g p t) -> p b g t", p=P, t=4))
        load_kv0(1)
        load_q(0, 1)
        load_kv(0, 1)
        load_wo(0)
        load_wo(1)
        load_q(1, 0)
        load_q(1, 1)
        load_kv(1, 0)
        load_kv(1, 1)

        def load_vec(i, v):
            nc.sync.dma_start(out=vec[i][0:8, :], in_=v.rearrange("(m n) -> m n", n=P))

        load_vec(0, bo)
        for h in range(2):
            load_audio(0, h)
        load_vec(1, gamma)
        load_vec(2, beta)
        for h in range(2):
            load_audio(1, h)
        ks_f = const.tile([P, 16], F32, name="ks_f")
        eps = const.tile([P, 2], F32, name="eps")
        nc.gpsimd.tensor_scalar(out=eps[:, 0:1], in0=id_f[:, 0:1], scalar1=0.0, scalar2=1e-6, op0=ALU.mult, op1=ALU.add)
        nc.gpsimd.tensor_scalar(out=eps[:, 1:2], in0=id_f[:, 0:1], scalar1=0.0, scalar2=1e-5, op0=ALU.mult, op1=ALU.add)
        nc.gpsimd.tensor_copy(out=ks_f[:], in_=ks_b[:])

        gq, qc, qs, xq = {}, {}, {}, {}
        for b in range(2):
            gq[b] = const.tile([P, 4096], BF16, name="gq%d" % b, align_bytes=64)

        def tqP(b, h, g):
            xt = rot(psum, [P, 2, 2, P], F32, "bank", 6)
            xq[b, h, g] = xt
            for n in range(2):
                w = words(q_raw[b, h][:, n, :])
                for u in range(2):
                    nc.tensor.transpose(xt[:, n, u, :], w[:, 256 * g + u : 256 * (g + 1) : 2], id_f[:])

        def tqS(b, h, g):
            o = 2048 * h + 1024 * g
            dst = words(gq[b][:, o : o + 1024]).rearrange("p (n r u) -> p n r u", n=2, u=2)
            nc.scalar.copy(out=dst, in_=xq[b, h, g][:].rearrange("p n u r -> p n r u"))

        def tqV(b, h, g):
            o = 2048 * h + 1024 * g
            dst = words(gq[b][:, o : o + 1024]).rearrange("p (n r u) -> p n r u", n=2, u=2)
            nc.vector.tensor_copy(out=dst, in_=xq[b, h, g][:].rearrange("p n u r -> p n r u"))

        def qq(b, h):
            qc[b, h] = rot(work, [P, 512], U32, "qc", 4, align_bytes=64)
            qs[b, h] = rot(work, [P, 512], U8, "qs", 4, align_bytes=64)
            nc.vector.quantize_mx(out=qc[b, h][:].bitcast(FP8X4), scales=qs[b, h][:], in_=gq[b][:, 2048 * h : 2048 * (h + 1)])

        kc, kss, grp, ibs = {}, {}, {}, {}

        def kv_dst(b, g, c):
            if (b, c) not in grp:
                grp[b, c] = rot(work, [P, 4096], BF16, "kvg", 2, align_bytes=64)
            return grp[b, c][:, 2048 * g : 2048 * (g + 1)]

        def kvV(b, g, c, k):
            dst = kv_dst(b, g, c).rearrange("p (t m j) -> p t m j", t=4, j=4)
            nc.vector.tensor_copy(out=dst, in_=kv_raw[b, g, c].rearrange("p j (m t) -> p t m j", t=4))

        def kvD(b, g, c, k):
            dst = kv_dst(b, g, c).rearrange("p (t m j) -> p t m j", t=4, j=4)
            src = kv_raw[b, g, c].rearrange("p j (m t) -> p t m j", t=4)
            nc.vector.tensor_copy(out=dst[:, 2 * k : 2 * k + 2], in_=src[:, 2 * k : 2 * k + 2])

        def kvP(b, g, c, k):
            if (b, g, c, k) not in ibs:
                ibs[b, g, c, k] = rot(psum, [P, D], BF16, "bank", 6)
            ib = ibs[b, g, c, k]
            src = kv_raw[b, g, c].rearrange("p j (m t) -> p t m j", t=4)
            for t in range(2):
                nc.tensor.matmul(ib[:, 512 * t : 512 * (t + 1)], id_b[:], src[:, 2 * k + t], start=True, stop=True)

        def kvE(b, g, c, k):
            nc.scalar.copy(out=kv_dst(b, g, c)[:, 1024 * k : 1024 * (k + 1)], in_=ibs[b, g, c, k][:])

        def kq(b, c):
            kc[b, c] = rot(work, [P, D], U32, "kc", 4, align_bytes=64)
            kss[b, c] = rot(work, [P, D], U8, "kss", 4, align_bytes=64)
            nc.vector.quantize_mx(out=kc[b, c][:].bitcast(FP8X4), scales=kss[b, c][:], in_=grp[b, c][:])

        rr = {}

        def arsH(b, G, t, h):
            if (b, h) not in rr:
                rr[b, h] = rot(work, [P, 8, 256], F32, "rr", 3)
            v = gq[b][:].rearrange("p (h g n j) -> p h g n j", h=2, g=2, j=4)
            i = 4 * G + t
            nc.scalar.activation(out=rr[b, h][:, i, :], in_=v[:, h, G, :, t], func=ACT.Abs_reciprocal_sqrt, bias=eps[:, 0:1], scale=ks_f[:, 8 * b + i : 8 * b + i + 1])

        def sq(b, h):
            r = rr[b, h][:]
            nc.scalar.activation(out=r, in_=r, func=ACT.Square)

        at, ac, acs, num = {}, {}, {}, {}

        def s1(b, n, G):
            num[b, n, G] = rot(psum, [P, 4, P], F32, "bank", 6)
            for t in range(4):
                for g in range(2):
                    cs = slice(512 * g + P * t, 512 * g + P * (t + 1))
                    o = 256 * g + P * (n % 2)
                    nc.tensor.matmul_mx(out=num[b, n, G][:, t, :], lhsT=kc[b, G][:, cs].bitcast(FP8X4), lhsT_scale=kss[b, G][:, cs], rhs=qc[b, n // 2][:, o : o + P].bitcast(FP8X4), rhs_scale=qs[b, n // 2][:, o : o + P], start=(g == 0), stop=(g == 1))

        def mul(b, n, G):
            ns = slice(P * (n % 2), P * (n % 2 + 1))
            if (b, n // 2) not in at:
                at[b, n // 2] = rot(work, [P, 2048], BF16, "at", 2, align_bytes=64)
            o = 1024 * G + 512 * (n % 2)
            nc.vector.tensor_tensor(out=at[b, n // 2][:, o : o + 512].rearrange("p (n j) -> p n j", j=4), in0=num[b, n, G][:].rearrange("p j n -> p n j"), in1=rr[b, n // 2][:, 4 * G : 4 * (G + 1), ns].rearrange("p j n -> p n j"), op=ALU.mult)

        def aq(b, h):
            ac[b, h] = rot(work, [P, 512], U32, "ac", 4, align_bytes=64)
            acs[b, h] = rot(work, [P, 512], U8, "acs", 4, align_bytes=64)
            nc.vector.quantize_mx(out=ac[b, h][:].bitcast(FP8X4), scales=acs[b, h][:], in_=at[b, h][:])

        gam = psum.tile([P, D], BF16, name="gam", bufs=1)
        bet = psum.tile([P, D], BF16, name="bet", bufs=1)
        spr = {}
        sc_bc = const.tile([P, D], F32, name="sc_bc")

        def spsP(h):
            spr[h] = rot(psum, [P, 512], F32, "bank", 6)
            for m in range(4):
                nc.tensor.transpose(spr[h][:, P * m : P * (m + 1)], scol[:, 4 * h + m : 4 * h + m + 1].to_broadcast([P, P]), id_f[:])

        def spsS(h):
            nc.scalar.copy(out=sc_bc[:, 512 * h : 512 * (h + 1)], in_=spr[h][:])


        bo_bc = const.tile([P, D], BF16, name="bo_bc")
        be_bc = const.tile([P, D], BF16, name="be_bc")

        def vecP(i):
            spr["t", i] = rot(psum, [P, P], BF16, "bank", 6)
            nc.tensor.transpose(spr["t", i][:], vec[i][:], id_b[:])

        def vecS(i):
            nc.scalar.copy(out=vcol[:, 8 * i : 8 * (i + 1)], in_=spr["t", i][:, 0:8])

        def spread(i):
            vb = (None, gam, bet)[i] if i else rot(psum, [P, D], BF16, "bank", 6)
            for m in range(8):
                nc.tensor.transpose(vb[:, P * m : P * (m + 1)], vcol[:, 8 * i + m : 8 * i + m + 1].to_broadcast([P, P]), id_b[:])
            spr["v", i] = vb

        def spreadS(i):
            nc.scalar.copy(out=(bo_bc, None, be_bc)[i][:], in_=spr["v", i][:])

        wc, wsc, gw, wb = {}, {}, {}, {}

        def wo(r):
            wb[r] = rot(work, [P, D], BF16, "wb", 4)
            nc.vector.tensor_tensor(out=wb[r][:], in0=wo8[r // 4][:, r % 4, :].bitcast(FP8), in1=sc_bc[:], op=ALU.mult)

        def twP(rp, G):
            xt = rot(psum, [P, 2, 2, P], F32, "bank", 6)
            xq[rp, G] = xt
            for k in range(2):
                for u in range(2):
                    nc.tensor.transpose(xt[:, k, u, :], words(wb[2 * rp + k][:])[:, 256 * G + u : 256 * (G + 1) : 2], id_f[:])

        def tw_dst(rp, G):
            h, i = rp // 2, rp % 2
            if h not in gw:
                gw[h] = work.tile([P, 4096], BF16, name="gw", bufs=1, align_bytes=64)
            o = 2048 * G + 1024 * i
            return words(gw[h][:, o : o + 1024]).rearrange("p (n r u) -> p n r u", n=2, u=2), xq[rp, G][:].rearrange("p n u r -> p n r u")

        def twS(rp, G):
            o, i = tw_dst(rp, G)
            nc.scalar.copy(out=o, in_=i)

        def wq(h):
            wc[h] = const.tile([P, D], U32, name="wc%d" % h, align_bytes=64)
            wsc[h] = const.tile([P, D], U8, name="wsc%d" % h, align_bytes=64)
            nc.vector.quantize_mx(out=wc[h][:].bitcast(FP8X4), scales=wsc[h][:], in_=gw[h][:])

        aa, z = {}, {}

        def res(b, n):
            if (b, n) not in aa:
                aa[b, n] = rot(work, [P, D], F32, "aa", 4)
            nc.gpsimd.tensor_tensor(out=aa[b, n][:], in0=au_raw[b, n], in1=bo_bc[:], op=ALU.add)

        def zP(b, n):
            for h in range(2):
                hs = slice(512 * h, 512 * (h + 1))
                z[b, n, h] = rot(psum, [P, 512], F32, "bank", 6)
                nc.tensor.matmul(z[b, n, h][:], id_b[:], au_raw[b, n][:, hs], start=True, stop=False)
                nc.tensor.matmul(z[b, n, h][:], id_b[:], bo_bc[:, hs], start=False, stop=True)

        def zS(b, n):
            if (b, n) not in aa:
                aa[b, n] = rot(work, [P, D], F32, "aa", 4)
            for h in range(2):
                nc.scalar.copy(out=aa[b, n][:, 512 * h : 512 * (h + 1)], in_=z[b, n, h][:])

        y, x, xn, st, sv = {}, {}, {}, {}, {}

        def s2(b, n):
            o = P * (n % 2)
            for h in range(2):
                y[b, n, h] = rot(psum, [P, 512], F32, "bank", 6)
                for G in range(2):
                    ts = slice(256 * G + o, 256 * G + o + P)
                    ws = slice(512 * G, 512 * (G + 1))
                    nc.tensor.matmul_mx(out=y[b, n, h][:], lhsT=ac[b, n // 2][:, ts].bitcast(FP8X4), lhsT_scale=acs[b, n // 2][:, ts], rhs=wc[h][:, ws].bitcast(FP8X4), rhs_scale=wsc[h][:, ws], start=(G == 0), stop=(G == 1))

        def addx(b, n):
            x[b, n] = rot(work, [P, D], F32, "x", 3)
            st[b, n] = rot(work, [P, 8], F32, "st", 4)
            for h in range(2):
                hs = slice(512 * h, 512 * (h + 1))
                nc.vector.scalar_tensor_tensor(out=x[b, n][:, hs], in0=y[b, n, h][:], scalar=1.0, in1=aa[b, n][:, hs], op0=ALU.mult, op1=ALU.add, accum_out=st[b, n][:, h : h + 1])

        def nmu(b, n):
            nc.vector.tensor_scalar(out=st[b, n][:, 2:3], in0=st[b, n][:, 0:1], scalar1=st[b, n][:, 1:2], scalar2=-1.0 / D, op0=ALU.add, op1=ALU.mult)

        def nmuS(b, n):
            nc.scalar.activation(out=st[b, n][:, 3:5], in_=st[b, n][:, 0:2], func=ACT.Copy, scale=-1.0 / D, accum_out=st[b, n][:, 2:3])

        def var(b, n):
            sv[b, n] = rot(work, [P, 8], F32, "sv", 4)
            junk = work.tile([P, D], BF16, name="junk", bufs=1)
            nc.scalar.activation(out=junk[:], in_=x[b, n][:], func=ACT.Square, bias=st[b, n][:, 2:3], accum_out=sv[b, n][:, 0:1])

        def rstd(b, n):
            nc.scalar.activation(out=sv[b, n][:, 1:2], in_=sv[b, n][:, 0:1], func=ACT.Abs_reciprocal_sqrt, bias=eps[:, 1:2], scale=1.0 / D)

        def cgam(b, n):
            if (b, n) not in xn:
                xn[b, n] = rot(work, [P, D], F32, "xn", 4)
            nc.vector.scalar_tensor_tensor(out=xn[b, n][:], in0=x[b, n][:], scalar=st[b, n][:, 2:3], in1=gam[:], op0=ALU.add, op1=ALU.mult)

        def srs(b, n):
            nc.scalar.activation(out=xn[b, n][:], in_=xn[b, n][:], func=ACT.Copy, scale=sv[b, n][:, 1:2])

        def dbeta(b, n):
            nc.gpsimd.tensor_tensor(out=xn[b, n][:], in0=xn[b, n][:], in1=be_bc[:], op=ALU.add)

        def dV(b, n):
            nc.vector.scalar_tensor_tensor(out=xn[b, n][:], in0=xn[b, n][:], scalar=sv[b, n][:, 1:2], in1=bet[:], op0=ALU.mult, op1=ALU.add)

        def dVh(b, n, h):
            hs = slice(512 * h, 512 * (h + 1))
            nc.vector.scalar_tensor_tensor(out=xn[b, n][:, hs], in0=xn[b, n][:, hs], scalar=sv[b, n][:, 1:2], in1=bet[:, hs], op0=ALU.mult, op1=ALU.add)

        def rows(b, n):
            h, i = n // 2, n % 2
            return out[b, 256 * h : 256 * (h + 1), :].rearrange("(p n) k -> n p k", n=2)[i]

        def storeh(b, n, h):
            hs = slice(512 * h, 512 * (h + 1))
            nc.sync.dma_start(out=rows(b, n)[:, hs], in_=xn[b, n][:, hs])

        def store(b, n):
            nc.sync.dma_start(out=rows(b, n), in_=xn[b, n][:])

        spsP(1)
        spsP(0)
        tqP(0, 0, 0)
        spsS(1)
        tqP(0, 0, 1)
        spsS(0)
        tqP(0, 1, 1)
        kvV(0, 0, 0, 0)
        tqS(0, 0, 0)
        arsH(0, 0, 2, 0)
        kvV(0, 0, 1, 0)
        tqP(0, 1, 0)
        tqS(0, 0, 1)
        arsH(0, 0, 3, 0)
        kvP(0, 1, 1, 0)
        arsH(0, 1, 1, 0)
        arsH(0, 1, 2, 0)
        qq(0, 0)
        arsH(0, 1, 0, 0)
        kvP(0, 1, 1, 1)
        tqV(0, 1, 1)
        kvV(0, 1, 0, 0)
        arsH(0, 1, 0, 1)
        arsH(0, 1, 3, 0)
        tqS(0, 1, 0)
        qq(0, 1)
        arsH(0, 0, 1, 0)
        wo(0)
        wo(1)
        wo(3)
        arsH(0, 0, 0, 0)
        twP(0, 0)
        arsH(0, 1, 1, 1)
        arsH(0, 0, 2, 1)
        arsH(0, 1, 3, 1)
        arsH(0, 0, 1, 1)
        sq(0, 0)
        twP(0, 1)
        wo(2)
        tqP(1, 1, 1)
        kq(0, 0)
        kvE(0, 1, 1, 0)
        kvE(0, 1, 1, 1)
        wo(5)
        tqP(1, 1, 0)
        twS(0, 0)
        twP(1, 1)
        kvD(1, 0, 1, 0)
        twP(1, 0)
        arsH(0, 0, 0, 1)
        wo(6)
        tqS(1, 1, 1)
        tqS(1, 1, 0)
        twS(0, 1)
        kq(0, 1)
        tqP(1, 0, 0)
        wo(7)
        arsH(1, 0, 1, 1)
        vecP(0)
        twS(1, 0)
        tqP(1, 0, 1)
        twS(1, 1)
        vecS(0)
        arsH(1, 1, 1, 1)
        s1(0, 1, 1)
        arsH(1, 0, 0, 1)
        tqS(1, 0, 1)
        arsH(1, 1, 2, 1)
        s1(0, 1, 0)
        arsH(1, 0, 3, 1)
        tqS(1, 0, 0)
        spread(0)
        wq(0)
        s1(0, 0, 1)
        arsH(0, 0, 3, 1)
        arsH(1, 1, 0, 1)
        arsH(0, 1, 2, 1)
        s1(0, 0, 0)
        s1(0, 2, 0)
        kvD(1, 0, 0, 0)
        s1(0, 3, 0)
        wo(4)
        kvV(1, 1, 0, 0)
        twP(2, 1)
        arsH(1, 1, 3, 1)
        spreadS(0)
        sq(0, 1)
        arsH(1, 0, 2, 1)
        mul(0, 1, 1)
        mul(0, 1, 0)
        twP(3, 0)
        twS(2, 1)
        s1(0, 3, 1)
        s1(0, 2, 1)
        vecP(1)
        arsH(1, 1, 1, 0)
        mul(0, 0, 1)
        mul(0, 0, 0)
        mul(0, 2, 0)
        arsH(1, 0, 0, 0)
        twS(3, 0)
        mul(0, 3, 0)
        vecS(1)
        arsH(1, 0, 2, 0)
        arsH(1, 0, 1, 0)
        arsH(1, 1, 0, 0)
        mul(0, 3, 1)
        arsH(1, 1, 3, 0)
        arsH(1, 1, 2, 0)
        mul(0, 2, 1)
        aq(0, 0)
        kvP(1, 0, 1, 1)
        twP(3, 1)
        kvE(1, 0, 1, 1)
        twP(2, 0)
        twS(2, 0)
        qq(1, 1)
        kvP(1, 0, 0, 1)
        twS(3, 1)
        kvV(1, 1, 1, 0)
        aq(0, 1)
        res(0, 3)
        vecP(2)
        kvE(1, 0, 0, 1)
        vecS(2)
        zP(0, 2)
        kq(1, 1)
        wq(1)
        zS(0, 2)
        zP(0, 1)
        s2(0, 3)
        kq(1, 0)
        zS(0, 1)
        addx(0, 3)
        s2(0, 2)
        sq(1, 1)
        s1(1, 2, 0)
        s2(0, 1)
        nmuS(0, 3)
        arsH(1, 0, 3, 0)
        s1(1, 3, 1)
        s1(1, 3, 0)
        qq(1, 0)
        spread(1)
        addx(0, 2)
        addx(0, 1)
        mul(1, 3, 1)
        mul(1, 2, 0)
        nmuS(0, 2)
        var(0, 3)
        s1(1, 2, 1)
        nmuS(0, 1)
        cgam(0, 3)
        rstd(0, 3)
        var(0, 1)
        s2(0, 0)
        sq(1, 0)
        s1(1, 1, 1)
        var(0, 2)
        s1(1, 0, 1)
        srs(0, 3)
        mul(1, 3, 0)
        mul(1, 2, 1)
        res(0, 0)
        res(1, 3)
        res(1, 2)
        addx(0, 0)
        aq(1, 1)
        mul(1, 0, 1)
        s1(1, 1, 0)
        nmuS(0, 0)
        rstd(0, 2)
        spread(2)
        mul(1, 1, 0)
        s1(1, 0, 0)
        mul(1, 0, 0)
        s2(1, 3)
        res(1, 0)
        mul(1, 1, 1)
        res(1, 1)
        cgam(0, 2)
        cgam(0, 0)
        aq(1, 0)
        spreadS(2)
        var(0, 0)
        rstd(0, 0)
        cgam(0, 1)
        rstd(0, 1)
        s2(1, 2)
        s2(1, 0)
        srs(0, 2)
        addx(1, 0)
        addx(1, 2)
        srs(0, 0)
        srs(0, 1)
        nmuS(1, 0)
        dbeta(0, 3)
        addx(1, 3)
        var(1, 0)
        dbeta(0, 2)
        nmuS(1, 2)
        s2(1, 1)
        var(1, 2)
        cgam(1, 0)
        cgam(1, 2)
        rstd(1, 0)
        addx(1, 1)
        nmuS(1, 3)
        rstd(1, 2)
        srs(1, 0)
        cgam(1, 3)
        dbeta(0, 0)
        dbeta(0, 1)
        nmu(1, 1)
        var(1, 3)
        srs(1, 2)
        rstd(1, 3)
        store(0, 3)
        store(0, 2)
        dbeta(1, 0)
        store(0, 0)
        dVh(1, 3, 0)
        dVh(1, 3, 1)
        var(1, 1)
        store(0, 1)
        store(1, 0)
        rstd(1, 1)
        storeh(1, 3, 0)
        storeh(1, 3, 1)
        cgam(1, 1)
        dbeta(1, 2)
        dV(1, 1)
        store(1, 2)
        store(1, 1)
